import numpy as np
import ml_dtypes


def mxq(x, axis, fmt="e4m3"):
    dtype, down = {"e4m3": (ml_dtypes.float8_e4m3fn, 7), "e5m2": (ml_dtypes.float8_e5m2, 14)}[fmt]
    v = np.moveaxis(np.asarray(x, np.float32).astype(ml_dtypes.bfloat16).astype(np.float64), axis, -1)
    blocks = v.reshape(v.shape[:-1] + (-1, 32))
    amax = np.abs(blocks).max(-1, keepdims=True)
    byte = np.maximum(np.where(amax > 0, np.frexp(amax)[1] - 1 + 127, 0) - down, 1)
    scale = np.exp2(byte - 127.0)
    codes = (blocks / scale).astype(np.float32).astype(dtype).astype(np.float64)
    return np.moveaxis((codes * scale).reshape(v.shape), -1, axis)


WIDE = False


def mx_kscale(k):
    if not WIDE:
        return np.ones(k)
    levels = np.array([10, -10, 5, -5, 0])
    a = np.random.permutation(np.resize(levels, k // 512 * 4)).reshape(k // 512, 4)
    idx = np.arange(k)
    return np.exp2(a[idx // 512, idx % 128 // 32])


BF16 = ml_dtypes.bfloat16


def bf(x):
    return np.asarray(x, np.float32).astype(BF16)


def f64(x):
    return np.asarray(x).astype(np.float64)


B, IN, OUT, G, P = 8192, 64, 256, 5, 3
NB = G + P
K = IN * NB
LO, HI = -1.0, 1.0
XE = 2.1875


def make_grid():
    gap = (HI - LO) / G
    g1d = np.arange(-P, G + P + 1) * gap + LO
    return np.broadcast_to(g1d, (IN, g1d.shape[0]))


def b_splines(x, grid):
    xg = x[:, :, None]
    bases = ((xg >= grid[:, :-1]) & (xg < grid[:, 1:])).astype(np.float64)
    for k in range(1, P + 1):
        left = (xg - grid[:, :-(k + 1)]) / (grid[:, k:-1] - grid[:, :-(k + 1)])
        right = (grid[:, k + 1:] - xg) / (grid[:, k + 1:] - grid[:, 1:-k])
        bases = left * bases[:, :, :-1] + right * bases[:, :, 1:]
    return bases


def setup_inputs():
    s = mx_kscale(K)
    edge = np.any(s != 1.0) & ((np.arange(IN) // (32 // NB)) % 2 == 1)
    x = np.random.standard_normal((B, IN))
    sign = np.where(np.random.standard_normal((B, IN)) < 0, -1.0, 1.0)
    x = np.where(edge[None, :], sign * XE, x)
    w = np.random.standard_normal((OUT, IN, NB)) * 3.2 / np.sqrt(IN)
    w = w * np.where(edge, 2.0 ** 18, 1.0)[None, :, None]
    return {"x": bf(x), "spline_weight": bf(w)}


def reference(x, spline_weight):
    grid = make_grid()
    bases = b_splines(f64(x), grid)
    bq = mxq(bases.reshape(B, K), 1, "e4m3")
    wq = mxq(f64(spline_weight).reshape(OUT, K), 1, "e4m3")
    return bq @ wq.T

@@ -1,0 +1,220 @@
+from contextlib import ExitStack
+
+import concourse.mybir as mybir
+from concourse.masks import make_identity
+
+F32 = mybir.dt.float32
+BF16 = mybir.dt.bfloat16
+U32 = mybir.dt.uint32
+U8 = mybir.dt.uint8
+FP8X4 = mybir.dt.float8_e4m3fn_x4
+ALU = mybir.AluOpType
+ACT = mybir.ActivationFunctionType
+AX = mybir.AxisListType
+
+P = 128
+B, IN, OUT, NB = 8192, 64, 256, 8
+K = IN * NB
+FLOPS = 2 * B * K * OUT
+T = B // P
+
+SIZES = (2, 2, 4, 8, 8, 8, 8, 8, 8, 4, 2, 2)
+LOADS = (4, 12, 16, 16, 16)
+D_ON_DVE = (0, 1)
+RG_ACT = 4
+MANUAL = True
+BIG_BUFS = 2
+
+
+def tile_kanlinearnores_v2_t_kernel(tc, x, spline_weight, out):
+    nc = tc.nc
+    x_v = x.rearrange("(p t) i -> p t i", t=T)
+    w_v = spline_weight.rearrange("(a p) i g -> p a (i g)", p=P)
+    out_v = out.rearrange("(p t) o -> p t o", t=T)
+    n_chunks = len(SIZES)
+    starts = [sum(SIZES[:c]) for c in range(n_chunks)]
+    assert sum(SIZES) == T and sum(LOADS) == T
+
+    with ExitStack() as ctx:
+        keep = ctx.enter_context(tc.tile_pool(name="keep", bufs=1))
+        xin = ctx.enter_context(tc.tile_pool(name="xin", bufs=3))
+        big = ctx.enter_context(tc.tile_pool(name="big", bufs=BIG_BUFS))
+        small = ctx.enter_context(tc.tile_pool(name="small", bufs=2))
+        xps_pool = ctx.enter_context(tc.psum_pool(name="xps", bufs=2))
+        wps_pool = ctx.enter_context(tc.psum_pool(name="wps", bufs=1))
+        ops_pool = ctx.enter_context(tc.psum_pool(name="ops", bufs=4))
+        if MANUAL:
+            ctx.enter_context(tc.manual_schedule())
+
+        x_nat = keep.tile([P, T, IN], BF16)
+        w_sb = keep.tile([P, 2, K], BF16)
+        lo = 0
+        for l, n in enumerate(LOADS):
+            nc.sync.dma_start(out=x_nat[:, lo:lo + n, :], in_=x_v[:, lo:lo + n, :])
+            lo += n
+            if l == 0:
+                nc.sync.dma_start(out=w_sb[:], in_=w_v)
+
+        ident = keep.tile([P, P], BF16)
+        make_identity(nc, ident[:])
+        j0 = keep.tile([P, 1], F32)
+        nc.vector.tensor_reduce(
+            out=j0[:],
+            in_=ident[:].rearrange("p (q j i) -> p q j i", q=16, j=2, i=4)[:, :, 1, :],
+            axis=AX.XY,
+            op=ALU.add,
+        )
+        cst = keep.tile([P, 4], F32)
+        for j1 in range(2):
+            nc.vector.tensor_scalar(out=cst[:, j1:j1 + 1], in0=j0[:], scalar1=-1.0, scalar2=1.5 - 2.0 * j1,
+                                    op0=ALU.mult, op1=ALU.add)
+            nc.vector.tensor_scalar(out=cst[:, 2 + j1:3 + j1], in0=j0[:], scalar1=0.4, scalar2=(2.0 * j1 - 1.5) * 0.4,
+                                    op0=ALU.mult, op1=ALU.add)
+
+        wcodes = keep.tile([P, OUT], U32, align_bytes=64)
+        wscales = keep.tile([P, OUT], U8, align_bytes=64)
+
+        def weights():
+            wr = keep.tile([P, 2, 4, P], BF16)
+            for a in range(2):
+                src = w_sb[:, a, :].rearrange("p (q i s j) -> p s q j i", q=16, i=4, s=4, j=2)
+                for s in range(4):
+                    nc.vector.tensor_copy(
+                        out=wr[:, a, s, :].rearrange("p (q j i) -> p q j i", q=16, j=2, i=4),
+                        in_=src[:, s],
+                    )
+            wps = wps_pool.tile([P, 4, OUT], BF16)
+            for a in range(2):
+                for s in range(4):
+                    nc.tensor.transpose(wps[:, s, a * P:(a + 1) * P], wr[:, a, s, :], ident[:])
+            wg = keep.tile([P, OUT, 4], BF16, align_bytes=64)
+            nc.vector.tensor_copy(out=wg[:], in_=wps[:].rearrange("p s o -> p o s"))
+            nc.vector.quantize_mx(out=wcodes[:].bitcast(FP8X4), scales=wscales[:],
+                                  in_=wg[:].rearrange("p o s -> p (o s)"))
+
+        st = {}
+
+        def ok(c):
+            return 0 <= c < n_chunks
+
+        def stage_x(c):
+            if not ok(c):
+                return
+            t0, n = starts[c], SIZES[c]
+            x2 = xin.tile([P, n, P], BF16, name="x2", tag="x2")
+            nc.vector.tensor_scalar(
+                out=x2[:].rearrange("p t (q j i) -> p (t q) j i", q=16, j=2, i=4),
+                in0=x_nat[:, t0:t0 + n, :].rearrange("p t (q i) -> p (t q) i", i=4).unsqueeze(2).to_broadcast([P, n * 16, 2, 4]),
+                scalar1=-4.0, scalar2=4.0, op0=ALU.max, op1=ALU.min,
+            )
+            xps = xps_pool.tile([P, n, P], BF16, name="xps", tag="xps")
+            for t in range(n):
+                nc.tensor.transpose(xps[:, t, :], x2[:, t, :], ident[:])
+            st[("xps", c)] = xps
+
+        def stage_a(c):
+            if not ok(c):
+                return
+            cols = SIZES[c] * P
+            xt = xin.tile([P, cols], BF16, name="xt", tag="xt")
+            nc.scalar.copy(out=xt[:], in_=st[("xps", c)][:].rearrange("p t b -> p (t b)"))
+            w = big.tile([P, 2, cols], F32, name="w", tag="w")
+            for j1 in range(2):
+                nc.scalar.activation(out=w[:, j1, :], in_=xt[:], func=ACT.Abs, bias=cst[:, j1:j1 + 1], scale=2.5)
+            a_ = big.tile([P, 2, cols], F32, name="a", tag="a")
+            nc.scalar.activation(out=a_[:], in_=w[:], func=ACT.Abs, bias=-2.0, scale=1.0)
+            d = big.tile([P, 2, cols], F32, name="d", tag="d")
+            if c not in D_ON_DVE:
+                nc.scalar.activation(out=d[:], in_=a_[:], func=ACT.Relu, bias=2.0, scale=-1.0)
+            sq = big.tile([P, 2, cols], F32, name="sq", tag="sq")
+            nc.scalar.activation(out=sq[:], in_=a_[:], func=ACT.Square, bias=2.0, scale=-1.0)
+            st[("xt", c)], st[("w", c)], st[("a", c)], st[("d", c)], st[("sq", c)] = xt, w, a_, d, sq
+
+        def stage_h(c):
+            if not ok(c):
+                return
+            cols = SIZES[c] * P
+            w, a_, d, sq = st[("w", c)], st[("a", c)], st[("d", c)], st[("sq", c)]
+            sg = 1.0
+            if c in D_ON_DVE:
+                nc.vector.tensor_scalar(out=d[:], in0=a_[:], scalar1=2.0, scalar2=2.0, op0=ALU.min, op1=ALU.subtract)
+                sg = -1.0
+            nc.vector.scalar_tensor_tensor(out=w[:], in0=d[:], scalar=sg / 6.0, in1=sq[:], op0=ALU.mult, op1=ALU.mult)
+            for j1 in range(2):
+                nc.vector.scalar_tensor_tensor(out=a_[:, j1, :], in0=d[:, j1, :], scalar=-0.5 * sg, in1=sq[:, 1 - j1, :],
+                                               op0=ALU.mult, op1=ALU.mult)
+            v = small.tile([P, 2, cols], BF16, name="v", tag="v")
+            nc.vector.scalar_tensor_tensor(out=v[:], in0=a_[:], scalar=2.0 / 3.0, in1=w[:], op0=ALU.add, op1=ALU.min)
+            st[("v", c)] = v
+
+        def stage_m(c):
+            if not ok(c):
+                return
+            cols = SIZES[c] * P
+            xt, v = st[("xt", c)], st[("v", c)]
+            m1 = small.tile([P, 2, cols], BF16, name="m1", tag="m1")
+            for j1 in range(2):
+                nc.vector.tensor_scalar(out=m1[:, j1, :], in0=xt[:], scalar1=cst[:, 2 + j1:3 + j1], scalar2=None, op0=ALU.is_ge)
+            pq = small.tile([P, 4, cols], BF16, name="pq", tag="pq")
+            nc.vector.tensor_tensor(out=pq[:, 2:4, :], in0=v[:], in1=m1[:], op=ALU.mult)
+            nc.vector.tensor_tensor(out=pq[:, 0:2, :], in0=v[:], in1=pq[:, 2:4, :], op=ALU.subtract)
+            grouped = small.tile([P, cols, 4], BF16, name="grouped", tag="grouped", align_bytes=64)
+            cv = cols - (cols * RG_ACT) // 16
+            nc.vector.tensor_copy(out=grouped[:, 0:cv, :], in_=pq[:, :, 0:cv].rearrange("p s c -> p c s"))
+            st[("pq", c)], st[("grouped", c)] = pq, grouped
+
+        def stage_r(c):
+            if not ok(c) or RG_ACT == 0:
+                return
+            cols = SIZES[c] * P
+            cv = cols - (cols * RG_ACT) // 16
+            nc.scalar.copy(out=st[("grouped", c)][:, cv:cols, :], in_=st[("pq", c)][:, :, cv:cols].rearrange("p s c -> p c s"))
+
+        def stage_z(c):
+            if not ok(c):
+                return
+            n = SIZES[c]
+            cols = n * P
+            codes = small.tile([P, cols], U32, name="codes", tag="codes", align_bytes=64)
+            scales = small.tile([P, cols], U8, name="scales", tag="scales", align_bytes=64)
+            nc.vector.quantize_mx(out=codes[:].bitcast(FP8X4), scales=scales[:],
+                                  in_=st[("grouped", c)][:].rearrange("p c s -> p (c s)"))
+            banks = []
+            for h in range((n + 1) // 2):
+                ops = ops_pool.tile([P, 2, OUT], F32, name="ops", tag="ops")
+                for e in range(min(2, n - 2 * h)):
+                    t = 2 * h + e
+                    nc.tensor.matmul_mx(
+                        out=ops[:, e, :],
+                        lhsT=codes[:, t * P:(t + 1) * P].bitcast(FP8X4),
+                        lhsT_scale=scales[:, t * P:(t + 1) * P],
+                        rhs=wcodes[:].bitcast(FP8X4),
+                        rhs_scale=wscales[:],
+                        start=True,
+                        stop=True,
+                    )
+                banks.append(ops)
+            st[("banks", c)] = banks
+
+        def stage_e(c):
+            if not ok(c):
+                return
+            t0, n = starts[c], SIZES[c]
+            out_sb = small.tile([P, n, OUT], F32, name="out_sb", tag="out_sb")
+            for h, ops in enumerate(st[("banks", c)]):
+                m = min(2, n - 2 * h)
+                nc.scalar.copy(out=out_sb[:, 2 * h:2 * h + m, :], in_=ops[:, 0:m, :])
+            nc.sync.dma_start(out=out_v[:, t0:t0 + n, :], in_=out_sb[:])
+
+        stage_x(0)
+        stage_x(1)
+        weights()
+        stage_x(2)
+        for i in range(-2, n_chunks + 1):
+            stage_h(i + 1)
+            stage_z(i)
+            stage_a(i + 2)
+            stage_e(i)
+            stage_m(i + 1)
+            stage_r(i + 1)
+            stage_x(i + 3)

@@ -20,10 +20,10 @@ T = B // P
 
 SIZES = (2, 2, 4, 8, 8, 8, 8, 8, 8, 4, 2, 2)
 LOADS = (4, 12, 16, 16, 16)
+X_ON_DVE = (0, 1, 2)
 D_ON_DVE = (0, 1)
-RG_ACT = 4
+RG_ACT = {9: 8, 10: 16, 11: 16}
 MANUAL = True
-BIG_BUFS = 2
 
 
 def tile_kanlinearnores_v2_t_kernel(tc, x, spline_weight, out):
@@ -37,8 +37,8 @@ def tile_kanlinearnores_v2_t_kernel(tc, x, spline_weight, out):
 
     with ExitStack() as ctx:
         keep = ctx.enter_context(tc.tile_pool(name="keep", bufs=1))
-        xin = ctx.enter_context(tc.tile_pool(name="xin", bufs=3))
-        big = ctx.enter_context(tc.tile_pool(name="big", bufs=BIG_BUFS))
+        xin = ctx.enter_context(tc.tile_pool(name="xin", bufs=4))
+        big = ctx.enter_context(tc.tile_pool(name="big", bufs=3))
         small = ctx.enter_context(tc.tile_pool(name="small", bufs=2))
         xps_pool = ctx.enter_context(tc.psum_pool(name="xps", bufs=2))
         wps_pool = ctx.enter_context(tc.psum_pool(name="wps", bufs=1))
@@ -71,6 +71,11 @@ def tile_kanlinearnores_v2_t_kernel(tc, x, spline_weight, out):
             nc.vector.tensor_scalar(out=cst[:, 2 + j1:3 + j1], in0=j0[:], scalar1=0.4, scalar2=(2.0 * j1 - 1.5) * 0.4,
                                     op0=ALU.mult, op1=ALU.add)
 
+        def clamp(l):
+            lo = sum(LOADS[:l])
+            piece = x_nat[:, lo:lo + LOADS[l], :]
+            nc.vector.tensor_scalar(out=piece, in0=piece, scalar1=-4.0, scalar2=4.0, op0=ALU.max, op1=ALU.min)
+
         wcodes = keep.tile([P, OUT], U32, align_bytes=64)
         wscales = keep.tile([P, OUT], U8, align_bytes=64)
 
@@ -97,78 +102,99 @@ def tile_kanlinearnores_v2_t_kernel(tc, x, spline_weight, out):
         def ok(c):
             return 0 <= c < n_chunks
 
+        def regroup(copy, dst, src):
+            copy(out=dst.rearrange("p (c i) s -> p c s i", i=4), in_=src.rearrange("p s (c i) -> p c s i", i=4))
+
         def stage_x(c):
             if not ok(c):
                 return
             t0, n = starts[c], SIZES[c]
             x2 = xin.tile([P, n, P], BF16, name="x2", tag="x2")
-            nc.vector.tensor_scalar(
-                out=x2[:].rearrange("p t (q j i) -> p (t q) j i", q=16, j=2, i=4),
-                in0=x_nat[:, t0:t0 + n, :].rearrange("p t (q i) -> p (t q) i", i=4).unsqueeze(2).to_broadcast([P, n * 16, 2, 4]),
-                scalar1=-4.0, scalar2=4.0, op0=ALU.max, op1=ALU.min,
-            )
+            dst = x2[:].rearrange("p t (q j i) -> p (t q) j i", q=16, j=2, i=4)
+            src = x_nat[:, t0:t0 + n, :].rearrange("p t (q i) -> p (t q) i", i=4).unsqueeze(2).to_broadcast([P, n * 16, 2, 4])
+            if c in X_ON_DVE:
+                nc.vector.tensor_copy(out=dst, in_=src)
+            else:
+                nc.scalar.copy(out=dst, in_=src)
             xps = xps_pool.tile([P, n, P], BF16, name="xps", tag="xps")
             for t in range(n):
                 nc.tensor.transpose(xps[:, t, :], x2[:, t, :], ident[:])
             st[("xps", c)] = xps
 
-        def stage_a(c):
+        def stage_t(c):
             if not ok(c):
                 return
             cols = SIZES[c] * P
             xt = xin.tile([P, cols], BF16, name="xt", tag="xt")
             nc.scalar.copy(out=xt[:], in_=st[("xps", c)][:].rearrange("p t b -> p (t b)"))
+            st[("xt", c)] = xt
+
+        def stage_a(c):
+            if not ok(c):
+                return
+            cols = SIZES[c] * P
+            xt = st[("xt", c)]
             w = big.tile([P, 2, cols], F32, name="w", tag="w")
+            a_ = big.tile([P, 2, cols], F32, name="a", tag="a")
+            d = big.tile([P, 2, cols], F32, name="d", tag="d")
+            sq = big.tile([P, 2, cols], F32, name="sq", tag="sq")
             for j1 in range(2):
                 nc.scalar.activation(out=w[:, j1, :], in_=xt[:], func=ACT.Abs, bias=cst[:, j1:j1 + 1], scale=2.5)
-            a_ = big.tile([P, 2, cols], F32, name="a", tag="a")
-            nc.scalar.activation(out=a_[:], in_=w[:], func=ACT.Abs, bias=-2.0, scale=1.0)
-            d = big.tile([P, 2, cols], F32, name="d", tag="d")
+            for j1 in range(2):
+                nc.scalar.activation(out=a_[:, j1, :], in_=w[:, j1, :], func=ACT.Abs, bias=-2.0, scale=1.0)
+            for j1 in range(2):
+                nc.scalar.activation(out=sq[:, j1, :], in_=a_[:, j1, :], func=ACT.Square, bias=2.0, scale=-1.0)
             if c not in D_ON_DVE:
-                nc.scalar.activation(out=d[:], in_=a_[:], func=ACT.Relu, bias=2.0, scale=-1.0)
-            sq = big.tile([P, 2, cols], F32, name="sq", tag="sq")
-            nc.scalar.activation(out=sq[:], in_=a_[:], func=ACT.Square, bias=2.0, scale=-1.0)
-            st[("xt", c)], st[("w", c)], st[("a", c)], st[("d", c)], st[("sq", c)] = xt, w, a_, d, sq
+                for j1 in range(2):
+                    nc.scalar.activation(out=d[:, j1, :], in_=a_[:, j1, :], func=ACT.Relu, bias=2.0, scale=-1.0)
+            st[("w", c)], st[("a", c)], st[("d", c)], st[("sq", c)] = w, a_, d, sq
 
         def stage_h(c):
             if not ok(c):
                 return
             cols = SIZES[c] * P
-            w, a_, d, sq = st[("w", c)], st[("a", c)], st[("d", c)], st[("sq", c)]
+            xt, w, a_, d, sq = st[("xt", c)], st[("w", c)], st[("a", c)], st[("d", c)], st[("sq", c)]
+            m1 = small.tile([P, 2, cols], BF16, name="m1", tag="m1")
+            v = small.tile([P, 2, cols], BF16, name="v", tag="v")
+            pq = small.tile([P, 4, cols], BF16, name="pq", tag="pq")
             sg = 1.0
             if c in D_ON_DVE:
-                nc.vector.tensor_scalar(out=d[:], in0=a_[:], scalar1=2.0, scalar2=2.0, op0=ALU.min, op1=ALU.subtract)
                 sg = -1.0
-            nc.vector.scalar_tensor_tensor(out=w[:], in0=d[:], scalar=sg / 6.0, in1=sq[:], op0=ALU.mult, op1=ALU.mult)
+                for j1 in range(2):
+                    nc.vector.tensor_scalar(out=d[:, j1, :], in0=a_[:, j1, :], scalar1=2.0, scalar2=2.0, op0=ALU.min, op1=ALU.subtract)
+            for j1 in range(2):
+                nc.vector.tensor_scalar(out=m1[:, j1, :], in0=xt[:], scalar1=cst[:, 2 + j1:3 + j1], scalar2=None, op0=ALU.is_ge)
             for j1 in range(2):
                 nc.vector.scalar_tensor_tensor(out=a_[:, j1, :], in0=d[:, j1, :], scalar=-0.5 * sg, in1=sq[:, 1 - j1, :],
                                                op0=ALU.mult, op1=ALU.mult)
-            v = small.tile([P, 2, cols], BF16, name="v", tag="v")
-            nc.vector.scalar_tensor_tensor(out=v[:], in0=a_[:], scalar=2.0 / 3.0, in1=w[:], op0=ALU.add, op1=ALU.min)
-            st[("v", c)] = v
+                nc.vector.scalar_tensor_tensor(out=w[:, j1, :], in0=d[:, j1, :], scalar=sg / 6.0, in1=sq[:, j1, :],
+                                               op0=ALU.mult, op1=ALU.mult)
+            for j1 in range(2):
+                nc.vector.scalar_tensor_tensor(out=v[:, j1, :], in0=a_[:, j1, :], scalar=2.0 / 3.0, in1=w[:, j1, :],
+                                               op0=ALU.add, op1=ALU.min)
+            for j1 in range(2):
+                nc.vector.tensor_tensor(out=pq[:, 2 + j1, :], in0=v[:, j1, :], in1=m1[:, j1, :], op=ALU.mult)
+            for j1 in range(2):
+                nc.vector.tensor_tensor(out=pq[:, j1, :], in0=v[:, j1, :], in1=pq[:, 2 + j1, :], op=ALU.subtract)
+            st[("pq", c)] = pq
 
         def stage_m(c):
             if not ok(c):
                 return
             cols = SIZES[c] * P
-            xt, v = st[("xt", c)], st[("v", c)]
-            m1 = small.tile([P, 2, cols], BF16, name="m1", tag="m1")
-            for j1 in range(2):
-                nc.vector.tensor_scalar(out=m1[:, j1, :], in0=xt[:], scalar1=cst[:, 2 + j1:3 + j1], scalar2=None, op0=ALU.is_ge)
-            pq = small.tile([P, 4, cols], BF16, name="pq", tag="pq")
-            nc.vector.tensor_tensor(out=pq[:, 2:4, :], in0=v[:], in1=m1[:], op=ALU.mult)
-            nc.vector.tensor_tensor(out=pq[:, 0:2, :], in0=v[:], in1=pq[:, 2:4, :], op=ALU.subtract)
+            pq = st[("pq", c)]
             grouped = small.tile([P, cols, 4], BF16, name="grouped", tag="grouped", align_bytes=64)
-            cv = cols - (cols * RG_ACT) // 16
-            nc.vector.tensor_copy(out=grouped[:, 0:cv, :], in_=pq[:, :, 0:cv].rearrange("p s c -> p c s"))
-            st[("pq", c)], st[("grouped", c)] = pq, grouped
+            cv = cols - (cols * RG_ACT.get(c, 0)) // 16
+            if cv:
+                regroup(nc.vector.tensor_copy, grouped[:, 0:cv, :], pq[:, :, 0:cv])
+            st[("grouped", c)] = grouped
 
         def stage_r(c):
-            if not ok(c) or RG_ACT == 0:
+            if not ok(c) or RG_ACT.get(c, 0) == 0:
                 return
             cols = SIZES[c] * P
-            cv = cols - (cols * RG_ACT) // 16
-            nc.scalar.copy(out=st[("grouped", c)][:, cv:cols, :], in_=st[("pq", c)][:, :, cv:cols].rearrange("p s c -> p c s"))
+            cv = cols - (cols * RG_ACT.get(c, 0)) // 16
+            regroup(nc.scalar.copy, st[("grouped", c)][:, cv:cols, :], st[("pq", c)][:, :, cv:cols])
 
         def stage_z(c):
             if not ok(c):
@@ -206,15 +232,24 @@ def tile_kanlinearnores_v2_t_kernel(tc, x, spline_weight, out):
                 nc.scalar.copy(out=out_sb[:, 2 * h:2 * h + m, :], in_=ops[:, 0:m, :])
             nc.sync.dma_start(out=out_v[:, t0:t0 + n, :], in_=out_sb[:])
 
+        clamp(0)
         stage_x(0)
+        clamp(1)
         stage_x(1)
-        weights()
+        stage_t(0)
+        stage_a(0)
         stage_x(2)
-        for i in range(-2, n_chunks + 1):
-            stage_h(i + 1)
-            stage_z(i)
-            stage_a(i + 2)
-            stage_e(i)
-            stage_m(i + 1)
-            stage_r(i + 1)
+        weights()
+        for l in range(2, len(LOADS)):
+            clamp(l)
+        stage_t(1)
+        stage_a(1)
+        for i in range(0, n_chunks + 3):
+            stage_t(i + 2)
             stage_x(i + 3)
+            stage_a(i + 2)
+            stage_e(i - 2)
+            stage_r(i - 1)
+            stage_h(i)
+            stage_z(i - 1)
+            stage_m(i)

@@ -18,12 +18,13 @@ K = IN * NB
 FLOPS = 2 * B * K * OUT
 T = B // P
 
-SIZES = (2, 2, 4, 8, 8, 8, 8, 8, 8, 4, 2, 2)
+SIZES = (2, 2, 4, 8, 8, 8, 8, 8, 8, 4, 4)
 LOADS = (4, 12, 16, 16, 16)
-X_ON_DVE = (0, 1, 2)
-D_ON_DVE = (0, 1)
-RG_ACT = {9: 8, 10: 16, 11: 16}
+X_ON_DVE = (2,)
+D_ON_DVE = ()
+RG_ACT = {7: 8, 8: 12, 9: 8}
 MANUAL = True
+PE_DUP = (3, 4, 5, 6, 7, 8)
 
 
 def tile_kanlinearnores_v2_t_kernel(tc, x, spline_weight, out):
@@ -41,7 +42,7 @@ def tile_kanlinearnores_v2_t_kernel(tc, x, spline_weight, out):
         big = ctx.enter_context(tc.tile_pool(name="big", bufs=3))
         small = ctx.enter_context(tc.tile_pool(name="small", bufs=2))
         xps_pool = ctx.enter_context(tc.psum_pool(name="xps", bufs=2))
-        wps_pool = ctx.enter_context(tc.psum_pool(name="wps", bufs=1))
+        ups_pool = ctx.enter_context(tc.psum_pool(name="ups", bufs=2))
         ops_pool = ctx.enter_context(tc.psum_pool(name="ops", bufs=4))
         if MANUAL:
             ctx.enter_context(tc.manual_schedule())
@@ -71,6 +72,13 @@ def tile_kanlinearnores_v2_t_kernel(tc, x, spline_weight, out):
             nc.vector.tensor_scalar(out=cst[:, 2 + j1:3 + j1], in0=j0[:], scalar1=0.4, scalar2=(2.0 * j1 - 1.5) * 0.4,
                                     op0=ALU.mult, op1=ALU.add)
 
+        sel = keep.tile([P, 2, P], BF16)
+        for tb in range(2):
+            nc.vector.tensor_copy(
+                out=sel[:, tb, :].rearrange("p (q j i) -> p q j i", q=16, j=2, i=4),
+                in_=ident[:, tb * IN:(tb + 1) * IN].rearrange("p (q i) -> p q i", i=4).unsqueeze(2).to_broadcast([P, 16, 2, 4]),
+            )
+
         def clamp(l):
             lo = sum(LOADS[:l])
             piece = x_nat[:, lo:lo + LOADS[l], :]
@@ -88,7 +96,7 @@ def tile_kanlinearnores_v2_t_kernel(tc, x, spline_weight, out):
                         out=wr[:, a, s, :].rearrange("p (q j i) -> p q j i", q=16, j=2, i=4),
                         in_=src[:, s],
                     )
-            wps = wps_pool.tile([P, 4, OUT], BF16)
+            wps = ups_pool.tile([P, 4, OUT], BF16, name="wps", tag="ups")
             for a in range(2):
                 for s in range(4):
                     nc.tensor.transpose(wps[:, s, a * P:(a + 1) * P], wr[:, a, s, :], ident[:])
@@ -105,20 +113,36 @@ def tile_kanlinearnores_v2_t_kernel(tc, x, spline_weight, out):
         def regroup(copy, dst, src):
             copy(out=dst.rearrange("p (c i) s -> p c s i", i=4), in_=src.rearrange("p s (c i) -> p c s i", i=4))
 
+        def stage_u(c):
+            if not ok(c) or c not in PE_DUP:
+                return
+            t0, n = starts[c], SIZES[c]
+            ups = ups_pool.tile([P, n // 2, P], BF16, name="ups", tag="ups")
+            for tp in range(n // 2):
+                nc.tensor.transpose(ups[:, tp, :], x_nat[:, t0 + 2 * tp:t0 + 2 * tp + 2, :].rearrange("p t i -> p (t i)"), ident[:])
+            st[("ups", c)] = ups
+
         def stage_x(c):
             if not ok(c):
                 return
             t0, n = starts[c], SIZES[c]
-            x2 = xin.tile([P, n, P], BF16, name="x2", tag="x2")
-            dst = x2[:].rearrange("p t (q j i) -> p (t q) j i", q=16, j=2, i=4)
-            src = x_nat[:, t0:t0 + n, :].rearrange("p t (q i) -> p (t q) i", i=4).unsqueeze(2).to_broadcast([P, n * 16, 2, 4])
-            if c in X_ON_DVE:
-                nc.vector.tensor_copy(out=dst, in_=src)
-            else:
-                nc.scalar.copy(out=dst, in_=src)
             xps = xps_pool.tile([P, n, P], BF16, name="xps", tag="xps")
-            for t in range(n):
-                nc.tensor.transpose(xps[:, t, :], x2[:, t, :], ident[:])
+            if c in PE_DUP:
+                xu = xin.tile([P, n // 2, P], BF16, name="xu", tag="xu")
+                nc.scalar.copy(out=xu[:], in_=st[("ups", c)][:])
+                for tb in range(2):
+                    nc.tensor.matmul(out=xps[:, tb * (n // 2):(tb + 1) * (n // 2), :].rearrange("p t b -> p (t b)"),
+                                     lhsT=sel[:, tb, :], rhs=xu[:].rearrange("p t b -> p (t b)"), start=True, stop=True)
+            else:
+                x2 = xin.tile([P, n, P], BF16, name="x2", tag="x2")
+                dst = x2[:].rearrange("p t (q j i) -> p (t q) j i", q=16, j=2, i=4)
+                src = x_nat[:, t0:t0 + n, :].rearrange("p t (q i) -> p (t q) i", i=4).unsqueeze(2).to_broadcast([P, n * 16, 2, 4])
+                if c in X_ON_DVE:
+                    nc.vector.tensor_copy(out=dst, in_=src)
+                else:
+                    nc.scalar.copy(out=dst, in_=src)
+                for t in range(n):
+                    nc.tensor.transpose(xps[:, t, :], x2[:, t, :], ident[:])
             st[("xps", c)] = xps
 
         def stage_t(c):
@@ -209,7 +233,7 @@ def tile_kanlinearnores_v2_t_kernel(tc, x, spline_weight, out):
             for h in range((n + 1) // 2):
                 ops = ops_pool.tile([P, 2, OUT], F32, name="ops", tag="ops")
                 for e in range(min(2, n - 2 * h)):
-                    t = 2 * h + e
+                    t = e * (n // 2) + h if c in PE_DUP else 2 * h + e
                     nc.tensor.matmul_mx(
                         out=ops[:, e, :],
                         lhsT=codes[:, t * P:(t + 1) * P].bitcast(FP8X4),
@@ -242,14 +266,16 @@ def tile_kanlinearnores_v2_t_kernel(tc, x, spline_weight, out):
         weights()
         for l in range(2, len(LOADS)):
             clamp(l)
+        stage_u(3)
         stage_t(1)
         stage_a(1)
         for i in range(0, n_chunks + 3):
             stage_t(i + 2)
             stage_x(i + 3)
+            stage_u(i + 4)
             stage_a(i + 2)
-            stage_e(i - 2)
             stage_r(i - 1)
+            stage_e(i - 2)
             stage_h(i)
             stage_z(i - 1)
             stage_m(i)

@@ -21,9 +21,10 @@ T = B // P
 SIZES = (2, 2, 4, 8, 8, 8, 8, 8, 8, 4, 4)
 LOADS = (4, 12, 16, 16, 16)
 X_ON_DVE = (2,)
-D_ON_DVE = ()
-RG_ACT = {7: 8, 8: 12, 9: 8}
+D_ON_DVE = (0, 1)
+RG_ACT = {7: 8, 8: 14, 9: 12}
 MANUAL = True
+E_DVE = {10: 1}
 PE_DUP = (3, 4, 5, 6, 7, 8)
 
 
@@ -87,7 +88,9 @@ def tile_kanlinearnores_v2_t_kernel(tc, x, spline_weight, out):
         wcodes = keep.tile([P, OUT], U32, align_bytes=64)
         wscales = keep.tile([P, OUT], U8, align_bytes=64)
 
-        def weights():
+        wps = ups_pool.tile([P, 4, OUT], BF16, name="wps", tag="ups")
+
+        def weights_1():
             wr = keep.tile([P, 2, 4, P], BF16)
             for a in range(2):
                 src = w_sb[:, a, :].rearrange("p (q i s j) -> p s q j i", q=16, i=4, s=4, j=2)
@@ -96,10 +99,11 @@ def tile_kanlinearnores_v2_t_kernel(tc, x, spline_weight, out):
                         out=wr[:, a, s, :].rearrange("p (q j i) -> p q j i", q=16, j=2, i=4),
                         in_=src[:, s],
                     )
-            wps = ups_pool.tile([P, 4, OUT], BF16, name="wps", tag="ups")
             for a in range(2):
                 for s in range(4):
                     nc.tensor.transpose(wps[:, s, a * P:(a + 1) * P], wr[:, a, s, :], ident[:])
+
+        def weights_2():
             wg = keep.tile([P, OUT, 4], BF16, align_bytes=64)
             nc.vector.tensor_copy(out=wg[:], in_=wps[:].rearrange("p s o -> p o s"))
             nc.vector.quantize_mx(out=wcodes[:].bitcast(FP8X4), scales=wscales[:],
@@ -253,7 +257,10 @@ def tile_kanlinearnores_v2_t_kernel(tc, x, spline_weight, out):
             out_sb = small.tile([P, n, OUT], F32, name="out_sb", tag="out_sb")
             for h, ops in enumerate(st[("banks", c)]):
                 m = min(2, n - 2 * h)
-                nc.scalar.copy(out=out_sb[:, 2 * h:2 * h + m, :], in_=ops[:, 0:m, :])
+                if h >= len(st[("banks", c)]) - E_DVE.get(c, 0):
+                    nc.vector.tensor_copy(out=out_sb[:, 2 * h:2 * h + m, :], in_=ops[:, 0:m, :])
+                else:
+                    nc.scalar.copy(out=out_sb[:, 2 * h:2 * h + m, :], in_=ops[:, 0:m, :])
             nc.sync.dma_start(out=out_v[:, t0:t0 + n, :], in_=out_sb[:])
 
         clamp(0)
@@ -263,7 +270,7 @@ def tile_kanlinearnores_v2_t_kernel(tc, x, spline_weight, out):
         stage_t(0)
         stage_a(0)
         stage_x(2)
-        weights()
+        weights_1()
         for l in range(2, len(LOADS)):
             clamp(l)
         stage_u(3)
@@ -277,5 +284,7 @@ def tile_kanlinearnores_v2_t_kernel(tc, x, spline_weight, out):
             stage_r(i - 1)
             stage_e(i - 2)
             stage_h(i)
+            if i == 0:
+                weights_2()
             stage_z(i - 1)
             stage_m(i)

@@ -10,7 +10,6 @@ U8 = mybir.dt.uint8
 FP8X4 = mybir.dt.float8_e4m3fn_x4
 ALU = mybir.AluOpType
 ACT = mybir.ActivationFunctionType
-AX = mybir.AxisListType
 
 P = 128
 B, IN, OUT, NB = 8192, 64, 256, 8
@@ -18,14 +17,9 @@ K = IN * NB
 FLOPS = 2 * B * K * OUT
 T = B // P
 
-SIZES = (2, 2, 4, 8, 8, 8, 8, 8, 8, 4, 4)
+SIZES = (2, 2, 4, 8, 8, 8, 8, 8, 8, 4, 2, 2)
 LOADS = (4, 12, 16, 16, 16)
-X_ON_DVE = (2,)
-D_ON_DVE = (0, 1)
-RG_ACT = {7: 8, 8: 14, 9: 12}
-MANUAL = True
-E_DVE = {10: 1}
-PE_DUP = (3, 4, 5, 6, 7, 8)
+HALF = K // 2
 
 
 def tile_kanlinearnores_v2_t_kernel(tc, x, spline_weight, out):
@@ -39,14 +33,13 @@ def tile_kanlinearnores_v2_t_kernel(tc, x, spline_weight, out):
 
     with ExitStack() as ctx:
         keep = ctx.enter_context(tc.tile_pool(name="keep", bufs=1))
-        xin = ctx.enter_context(tc.tile_pool(name="xin", bufs=4))
-        big = ctx.enter_context(tc.tile_pool(name="big", bufs=3))
+        act2 = ctx.enter_context(tc.tile_pool(name="act2", bufs=2))
+        act3 = ctx.enter_context(tc.tile_pool(name="act3", bufs=3))
+        dve = ctx.enter_context(tc.tile_pool(name="dve", bufs=2))
         small = ctx.enter_context(tc.tile_pool(name="small", bufs=2))
-        xps_pool = ctx.enter_context(tc.psum_pool(name="xps", bufs=2))
-        ups_pool = ctx.enter_context(tc.psum_pool(name="ups", bufs=2))
+        xt_pool = ctx.enter_context(tc.psum_pool(name="xtp", bufs=4))
         ops_pool = ctx.enter_context(tc.psum_pool(name="ops", bufs=4))
-        if MANUAL:
-            ctx.enter_context(tc.manual_schedule())
+        ctx.enter_context(tc.manual_schedule())
 
         x_nat = keep.tile([P, T, IN], BF16)
         w_sb = keep.tile([P, 2, K], BF16)
@@ -57,234 +50,179 @@ def tile_kanlinearnores_v2_t_kernel(tc, x, spline_weight, out):
             if l == 0:
                 nc.sync.dma_start(out=w_sb[:], in_=w_v)
 
-        ident = keep.tile([P, P], BF16)
-        make_identity(nc, ident[:])
-        j0 = keep.tile([P, 1], F32)
-        nc.vector.tensor_reduce(
-            out=j0[:],
-            in_=ident[:].rearrange("p (q j i) -> p q j i", q=16, j=2, i=4)[:, :, 1, :],
-            axis=AX.XY,
-            op=ALU.add,
-        )
-        cst = keep.tile([P, 4], F32)
-        for j1 in range(2):
-            nc.vector.tensor_scalar(out=cst[:, j1:j1 + 1], in0=j0[:], scalar1=-1.0, scalar2=1.5 - 2.0 * j1,
-                                    op0=ALU.mult, op1=ALU.add)
-            nc.vector.tensor_scalar(out=cst[:, 2 + j1:3 + j1], in0=j0[:], scalar1=0.4, scalar2=(2.0 * j1 - 1.5) * 0.4,
-                                    op0=ALU.mult, op1=ALU.add)
-
-        sel = keep.tile([P, 2, P], BF16)
-        for tb in range(2):
-            nc.vector.tensor_copy(
-                out=sel[:, tb, :].rearrange("p (q j i) -> p q j i", q=16, j=2, i=4),
-                in_=ident[:, tb * IN:(tb + 1) * IN].rearrange("p (q i) -> p q i", i=4).unsqueeze(2).to_broadcast([P, 16, 2, 4]),
-            )
+        identf = keep.tile([P, P], F32)
+        make_identity(nc, identf[:])
 
         def clamp(l):
             lo = sum(LOADS[:l])
             piece = x_nat[:, lo:lo + LOADS[l], :]
             nc.vector.tensor_scalar(out=piece, in0=piece, scalar1=-4.0, scalar2=4.0, op0=ALU.max, op1=ALU.min)
 
-        wcodes = keep.tile([P, OUT], U32, align_bytes=64)
-        wscales = keep.tile([P, OUT], U8, align_bytes=64)
-
-        wps = ups_pool.tile([P, 4, OUT], BF16, name="wps", tag="ups")
-
-        def weights_1():
-            wr = keep.tile([P, 2, 4, P], BF16)
-            for a in range(2):
-                src = w_sb[:, a, :].rearrange("p (q i s j) -> p s q j i", q=16, i=4, s=4, j=2)
-                for s in range(4):
-                    nc.vector.tensor_copy(
-                        out=wr[:, a, s, :].rearrange("p (q j i) -> p q j i", q=16, j=2, i=4),
-                        in_=src[:, s],
-                    )
-            for a in range(2):
-                for s in range(4):
-                    nc.tensor.transpose(wps[:, s, a * P:(a + 1) * P], wr[:, a, s, :], ident[:])
-
-        def weights_2():
-            wg = keep.tile([P, OUT, 4], BF16, align_bytes=64)
-            nc.vector.tensor_copy(out=wg[:], in_=wps[:].rearrange("p s o -> p o s"))
-            nc.vector.quantize_mx(out=wcodes[:].bitcast(FP8X4), scales=wscales[:],
-                                  in_=wg[:].rearrange("p o s -> p (o s)"))
-
         st = {}
 
         def ok(c):
             return 0 <= c < n_chunks
 
-        def regroup(copy, dst, src):
-            copy(out=dst.rearrange("p (c i) s -> p c s i", i=4), in_=src.rearrange("p s (c i) -> p c s i", i=4))
+        def x_of(c):
+            return x_nat[:, starts[c]:starts[c] + SIZES[c], :].rearrange("p t i -> p (t i)")
 
-        def stage_u(c):
-            if not ok(c) or c not in PE_DUP:
-                return
-            t0, n = starts[c], SIZES[c]
-            ups = ups_pool.tile([P, n // 2, P], BF16, name="ups", tag="ups")
-            for tp in range(n // 2):
-                nc.tensor.transpose(ups[:, tp, :], x_nat[:, t0 + 2 * tp:t0 + 2 * tp + 2, :].rearrange("p t i -> p (t i)"), ident[:])
-            st[("ups", c)] = ups
-
-        def stage_x(c):
+        def stage_1(c):
             if not ok(c):
                 return
-            t0, n = starts[c], SIZES[c]
-            xps = xps_pool.tile([P, n, P], BF16, name="xps", tag="xps")
-            if c in PE_DUP:
-                xu = xin.tile([P, n // 2, P], BF16, name="xu", tag="xu")
-                nc.scalar.copy(out=xu[:], in_=st[("ups", c)][:])
-                for tb in range(2):
-                    nc.tensor.matmul(out=xps[:, tb * (n // 2):(tb + 1) * (n // 2), :].rearrange("p t b -> p (t b)"),
-                                     lhsT=sel[:, tb, :], rhs=xu[:].rearrange("p t b -> p (t b)"), start=True, stop=True)
-            else:
-                x2 = xin.tile([P, n, P], BF16, name="x2", tag="x2")
-                dst = x2[:].rearrange("p t (q j i) -> p (t q) j i", q=16, j=2, i=4)
-                src = x_nat[:, t0:t0 + n, :].rearrange("p t (q i) -> p (t q) i", i=4).unsqueeze(2).to_broadcast([P, n * 16, 2, 4])
-                if c in X_ON_DVE:
-                    nc.vector.tensor_copy(out=dst, in_=src)
-                else:
-                    nc.scalar.copy(out=dst, in_=src)
-                for t in range(n):
-                    nc.tensor.transpose(xps[:, t, :], x2[:, t, :], ident[:])
-            st[("xps", c)] = xps
+            cols = SIZES[c] * IN
+            w = act2.tile([P, 4, cols], F32, name="w", tag="w")
+            a_ = act3.tile([P, 4, cols], F32, name="a", tag="a")
+            sq = act3.tile([P, 4, cols], F32, name="sq", tag="sq")
+            for r in range(4):
+                nc.scalar.activation(out=w[:, r, :], in_=x_of(c), func=ACT.Abs, bias=1.5 - r, scale=2.5)
+            for hf in range(2):
+                nc.scalar.activation(out=a_[:, 2 * hf:2 * hf + 2, :], in_=w[:, 2 * hf:2 * hf + 2, :], func=ACT.Abs, bias=-2.0, scale=1.0)
+            for hf in range(2):
+                nc.scalar.activation(out=sq[:, 2 * hf:2 * hf + 2, :], in_=a_[:, 2 * hf:2 * hf + 2, :], func=ACT.Square, bias=2.0, scale=-1.0)
+            st[("a", c)], st[("sq", c)] = a_, sq
 
-        def stage_t(c):
+        def stage_2a(c):
             if not ok(c):
                 return
-            cols = SIZES[c] * P
-            xt = xin.tile([P, cols], BF16, name="xt", tag="xt")
-            nc.scalar.copy(out=xt[:], in_=st[("xps", c)][:].rearrange("p t b -> p (t b)"))
-            st[("xt", c)] = xt
+            cols = SIZES[c] * IN
+            a_, sq = st[("a", c)], st[("sq", c)]
+            m = small.tile([P, 4, cols], BF16, name="m", tag="m")
+            v = small.tile([P, 4, cols], BF16, name="v", tag="v")
+            nd = dve.tile([P, 4, cols], F32, name="nd", tag="nd")
+            qa = dve.tile([P, 4, cols], F32, name="qa", tag="qa")
+            pa = dve.tile([P, 4, cols], F32, name="pa", tag="pa")
+            for r in range(4):
+                nc.vector.tensor_scalar(out=m[:, r, :], in0=x_of(c), scalar1=0.4 * (r - 1.5), scalar2=None, op0=ALU.is_ge)
+            halves = (slice(0, 2), slice(2, 4))
+            for hf in range(2):
+                nc.vector.tensor_scalar(out=nd[:, halves[hf], :], in0=a_[:, halves[hf], :], scalar1=2.0, scalar2=2.0,
+                                        op0=ALU.min, op1=ALU.subtract)
+            for hf in range(2):
+                nc.vector.scalar_tensor_tensor(out=qa[:, halves[hf], :], in0=nd[:, halves[hf], :], scalar=0.5,
+                                               in1=sq[:, halves[1 - hf], :], op0=ALU.mult, op1=ALU.mult)
+            for hf in range(2):
+                nc.vector.scalar_tensor_tensor(out=pa[:, halves[hf], :], in0=nd[:, halves[hf], :], scalar=-1.0 / 6.0,
+                                               in1=sq[:, halves[hf], :], op0=ALU.mult, op1=ALU.mult)
+            for hf in range(2):
+                nc.vector.scalar_tensor_tensor(out=v[:, halves[hf], :], in0=qa[:, halves[hf], :], scalar=2.0 / 3.0,
+                                               in1=pa[:, halves[hf], :], op0=ALU.add, op1=ALU.min)
+            st[("m", c)], st[("v", c)] = m, v
 
-        def stage_a(c):
-            if not ok(c):
-                return
-            cols = SIZES[c] * P
-            xt = st[("xt", c)]
-            w = big.tile([P, 2, cols], F32, name="w", tag="w")
-            a_ = big.tile([P, 2, cols], F32, name="a", tag="a")
-            d = big.tile([P, 2, cols], F32, name="d", tag="d")
-            sq = big.tile([P, 2, cols], F32, name="sq", tag="sq")
-            for j1 in range(2):
-                nc.scalar.activation(out=w[:, j1, :], in_=xt[:], func=ACT.Abs, bias=cst[:, j1:j1 + 1], scale=2.5)
-            for j1 in range(2):
-                nc.scalar.activation(out=a_[:, j1, :], in_=w[:, j1, :], func=ACT.Abs, bias=-2.0, scale=1.0)
-            for j1 in range(2):
-                nc.scalar.activation(out=sq[:, j1, :], in_=a_[:, j1, :], func=ACT.Square, bias=2.0, scale=-1.0)
-            if c not in D_ON_DVE:
-                for j1 in range(2):
-                    nc.scalar.activation(out=d[:, j1, :], in_=a_[:, j1, :], func=ACT.Relu, bias=2.0, scale=-1.0)
-            st[("w", c)], st[("a", c)], st[("d", c)], st[("sq", c)] = w, a_, d, sq
-
-        def stage_h(c):
-            if not ok(c):
-                return
-            cols = SIZES[c] * P
-            xt, w, a_, d, sq = st[("xt", c)], st[("w", c)], st[("a", c)], st[("d", c)], st[("sq", c)]
-            m1 = small.tile([P, 2, cols], BF16, name="m1", tag="m1")
-            v = small.tile([P, 2, cols], BF16, name="v", tag="v")
-            pq = small.tile([P, 4, cols], BF16, name="pq", tag="pq")
-            sg = 1.0
-            if c in D_ON_DVE:
-                sg = -1.0
-                for j1 in range(2):
-                    nc.vector.tensor_scalar(out=d[:, j1, :], in0=a_[:, j1, :], scalar1=2.0, scalar2=2.0, op0=ALU.min, op1=ALU.subtract)
-            for j1 in range(2):
-                nc.vector.tensor_scalar(out=m1[:, j1, :], in0=xt[:], scalar1=cst[:, 2 + j1:3 + j1], scalar2=None, op0=ALU.is_ge)
-            for j1 in range(2):
-                nc.vector.scalar_tensor_tensor(out=a_[:, j1, :], in0=d[:, j1, :], scalar=-0.5 * sg, in1=sq[:, 1 - j1, :],
-                                               op0=ALU.mult, op1=ALU.mult)
-                nc.vector.scalar_tensor_tensor(out=w[:, j1, :], in0=d[:, j1, :], scalar=sg / 6.0, in1=sq[:, j1, :],
-                                               op0=ALU.mult, op1=ALU.mult)
-            for j1 in range(2):
-                nc.vector.scalar_tensor_tensor(out=v[:, j1, :], in0=a_[:, j1, :], scalar=2.0 / 3.0, in1=w[:, j1, :],
-                                               op0=ALU.add, op1=ALU.min)
-            for j1 in range(2):
-                nc.vector.tensor_tensor(out=pq[:, 2 + j1, :], in0=v[:, j1, :], in1=m1[:, j1, :], op=ALU.mult)
-            for j1 in range(2):
-                nc.vector.tensor_tensor(out=pq[:, j1, :], in0=v[:, j1, :], in1=pq[:, 2 + j1, :], op=ALU.subtract)
-            st[("pq", c)] = pq
-
-        def stage_m(c):
-            if not ok(c):
-                return
-            cols = SIZES[c] * P
-            pq = st[("pq", c)]
-            grouped = small.tile([P, cols, 4], BF16, name="grouped", tag="grouped", align_bytes=64)
-            cv = cols - (cols * RG_ACT.get(c, 0)) // 16
-            if cv:
-                regroup(nc.vector.tensor_copy, grouped[:, 0:cv, :], pq[:, :, 0:cv])
-            st[("grouped", c)] = grouped
-
-        def stage_r(c):
-            if not ok(c) or RG_ACT.get(c, 0) == 0:
-                return
-            cols = SIZES[c] * P
-            cv = cols - (cols * RG_ACT.get(c, 0)) // 16
-            regroup(nc.scalar.copy, st[("grouped", c)][:, cv:cols, :], st[("pq", c)][:, :, cv:cols])
-
-        def stage_z(c):
+        def stage_2b(c):
             if not ok(c):
                 return
             n = SIZES[c]
-            cols = n * P
-            codes = small.tile([P, cols], U32, name="codes", tag="codes", align_bytes=64)
-            scales = small.tile([P, cols], U8, name="scales", tag="scales", align_bytes=64)
-            nc.vector.quantize_mx(out=codes[:].bitcast(FP8X4), scales=scales[:],
-                                  in_=st[("grouped", c)][:].rearrange("p c s -> p (c s)"))
+            m, v = st[("m", c)], st[("v", c)]
+            pq = small.tile([P, 2, n, HALF], BF16, name="pq", tag="pq")
+            vv = v[:].rearrange("p r (c i) -> p c r i", i=4)
+            mv = m[:].rearrange("p r (c i) -> p c r i", i=4)
+            hi = pq[:, 1].rearrange("p t (q r i) -> p (t q) r i", r=4, i=4)
+            lo_ = pq[:, 0].rearrange("p t (q r i) -> p (t q) r i", r=4, i=4)
+            nq = n * 16
+            parts = (slice(0, nq // 2), slice(nq // 2, nq))
+            for s in parts:
+                nc.vector.tensor_tensor(out=hi[:, s], in0=vv[:, s], in1=mv[:, s], op=ALU.mult)
+            for s in parts:
+                nc.vector.tensor_tensor(out=lo_[:, s], in0=vv[:, s], in1=hi[:, s], op=ALU.subtract)
+            st[("pq", c)] = pq
+
+        def stage_3(c):
+            if c not in st_n:
+                return
+            n, pq = st_n[c], st[("pq", c)]
             banks = []
-            for h in range((n + 1) // 2):
+            for j in range(n // 2):
+                xt = xt_pool.tile([P, 2, 2, P], F32, name="xt", tag="xt")
+                for t in range(2):
+                    for u in range(2):
+                        nc.tensor.transpose(xt[:, t, u, :], pq[:, u, 2 * j + t, :].bitcast(F32), identf[:])
+                banks.append(xt)
+            st[("xt", c)] = banks
+
+        def stage_4(c):
+            if c not in st_n:
+                return
+            n = st_n[c]
+            grouped = small.tile([P, n * K], BF16, name="grouped", tag="grouped", align_bytes=64)
+            g32 = grouped[:].bitcast(F32)
+            for j, xt in enumerate(st[("xt", c)]):
+                nc.scalar.copy(out=g32[:, j * K:(j + 1) * K].rearrange("p (t b u) -> p t b u", t=2, u=2),
+                               in_=xt[:].rearrange("p t u b -> p t b u"))
+            st[("grouped", c)] = grouped
+
+        def stage_5(c):
+            if c not in st_n:
+                return
+            n = st_n[c]
+            if c == "w":
+                codes = keep.tile([P, n * P], U32, name="wcodes", align_bytes=64)
+                scales = keep.tile([P, n * P], U8, name="wscales", align_bytes=64)
+            else:
+                codes = small.tile([P, n * P], U32, name="codes", tag="codes", align_bytes=64)
+                scales = small.tile([P, n * P], U8, name="scales", tag="scales", align_bytes=64)
+            nc.vector.quantize_mx(out=codes[:].bitcast(FP8X4), scales=scales[:], in_=st[("grouped", c)][:])
+            st[("codes", c)], st[("scales", c)] = codes, scales
+
+        def stage_6(c):
+            if not ok(c):
+                return
+            n = SIZES[c]
+            codes, scales = st[("codes", c)], st[("scales", c)]
+            banks = []
+            for j in range(n // 2):
                 ops = ops_pool.tile([P, 2, OUT], F32, name="ops", tag="ops")
-                for e in range(min(2, n - 2 * h)):
-                    t = e * (n // 2) + h if c in PE_DUP else 2 * h + e
+                for e in range(2):
+                    t = 2 * j + e
                     nc.tensor.matmul_mx(
                         out=ops[:, e, :],
                         lhsT=codes[:, t * P:(t + 1) * P].bitcast(FP8X4),
                         lhsT_scale=scales[:, t * P:(t + 1) * P],
-                        rhs=wcodes[:].bitcast(FP8X4),
-                        rhs_scale=wscales[:],
+                        rhs=st[("codes", "w")][:].bitcast(FP8X4),
+                        rhs_scale=st[("scales", "w")][:],
                         start=True,
                         stop=True,
                     )
                 banks.append(ops)
             st[("banks", c)] = banks
 
-        def stage_e(c):
+        def stage_7(c):
             if not ok(c):
                 return
             t0, n = starts[c], SIZES[c]
             out_sb = small.tile([P, n, OUT], F32, name="out_sb", tag="out_sb")
-            for h, ops in enumerate(st[("banks", c)]):
-                m = min(2, n - 2 * h)
-                if h >= len(st[("banks", c)]) - E_DVE.get(c, 0):
-                    nc.vector.tensor_copy(out=out_sb[:, 2 * h:2 * h + m, :], in_=ops[:, 0:m, :])
-                else:
-                    nc.scalar.copy(out=out_sb[:, 2 * h:2 * h + m, :], in_=ops[:, 0:m, :])
+            for j, ops in enumerate(st[("banks", c)]):
+                nc.scalar.copy(out=out_sb[:, 2 * j:2 * j + 2, :], in_=ops[:])
             nc.sync.dma_start(out=out_v[:, t0:t0 + n, :], in_=out_sb[:])
 
+        st_n = {"w": 2}
+        for c in range(n_chunks):
+            st_n[c] = SIZES[c]
+
+        def weights_rows():
+            wpq = keep.tile([P, 2, 2, HALF], BF16)
+            src = w_sb[:].rearrange("p a (q i h r) -> p h a q r i", q=16, i=4, h=2, r=4)
+            for h in range(2):
+                for a in range(2):
+                    nc.vector.tensor_copy(out=wpq[:, h, a, :].rearrange("p (q r i) -> p q r i", r=4, i=4), in_=src[:, h, a])
+            st[("pq", "w")] = wpq
+
         clamp(0)
-        stage_x(0)
+        stage_1(0)
+        weights_rows()
+        stage_3("w")
         clamp(1)
-        stage_x(1)
-        stage_t(0)
-        stage_a(0)
-        stage_x(2)
-        weights_1()
-        for l in range(2, len(LOADS)):
-            clamp(l)
-        stage_u(3)
-        stage_t(1)
-        stage_a(1)
-        for i in range(0, n_chunks + 3):
-            stage_t(i + 2)
-            stage_x(i + 3)
-            stage_u(i + 4)
-            stage_a(i + 2)
-            stage_r(i - 1)
-            stage_e(i - 2)
-            stage_h(i)
+        for i in range(0, n_chunks + 2):
+            stage_3(i - 1)
+            stage_6(i - 2)
+            stage_1(i + 1)
             if i == 0:
-                weights_2()
-            stage_z(i - 1)
-            stage_m(i)
+                stage_4("w")
+            stage_4(i - 1)
+            stage_7(i - 2)
+            stage_2a(i)
+            if i == 0:
+                stage_5("w")
+                for l in range(2, len(LOADS)):
+                    clamp(l)
+            stage_5(i - 1)
+            stage_2b(i)

@@ -19,6 +19,7 @@ T = B // P
 
 SIZES = (2, 2, 4, 8, 8, 8, 8, 8, 8, 4, 2, 2)
 LOADS = (4, 12, 16, 16, 16)
+D_ACT = (4, 6, 8)
 HALF = K // 2
 
 
@@ -39,7 +40,6 @@ def tile_kanlinearnores_v2_t_kernel(tc, x, spline_weight, out):
         small = ctx.enter_context(tc.tile_pool(name="small", bufs=2))
         xt_pool = ctx.enter_context(tc.psum_pool(name="xtp", bufs=4))
         ops_pool = ctx.enter_context(tc.psum_pool(name="ops", bufs=4))
-        ctx.enter_context(tc.manual_schedule())
 
         x_nat = keep.tile([P, T, IN], BF16)
         w_sb = keep.tile([P, 2, K], BF16)
@@ -79,6 +79,11 @@ def tile_kanlinearnores_v2_t_kernel(tc, x, spline_weight, out):
                 nc.scalar.activation(out=a_[:, 2 * hf:2 * hf + 2, :], in_=w[:, 2 * hf:2 * hf + 2, :], func=ACT.Abs, bias=-2.0, scale=1.0)
             for hf in range(2):
                 nc.scalar.activation(out=sq[:, 2 * hf:2 * hf + 2, :], in_=a_[:, 2 * hf:2 * hf + 2, :], func=ACT.Square, bias=2.0, scale=-1.0)
+            if c in D_ACT:
+                d = act3.tile([P, 4, cols], F32, name="d", tag="d")
+                for hf in range(2):
+                    nc.scalar.activation(out=d[:, 2 * hf:2 * hf + 2, :], in_=a_[:, 2 * hf:2 * hf + 2, :], func=ACT.Relu, bias=2.0, scale=-1.0)
+                st[("d", c)] = d
             st[("a", c)], st[("sq", c)] = a_, sq
 
         def stage_2a(c):
@@ -88,20 +93,26 @@ def tile_kanlinearnores_v2_t_kernel(tc, x, spline_weight, out):
             a_, sq = st[("a", c)], st[("sq", c)]
             m = small.tile([P, 4, cols], BF16, name="m", tag="m")
             v = small.tile([P, 4, cols], BF16, name="v", tag="v")
-            nd = dve.tile([P, 4, cols], F32, name="nd", tag="nd")
+            sg = 1.0
+            if c in D_ACT:
+                nd = st[("d", c)]
+                sg = -1.0
+            else:
+                nd = dve.tile([P, 4, cols], F32, name="nd", tag="nd")
             qa = dve.tile([P, 4, cols], F32, name="qa", tag="qa")
             pa = dve.tile([P, 4, cols], F32, name="pa", tag="pa")
             for r in range(4):
                 nc.vector.tensor_scalar(out=m[:, r, :], in0=x_of(c), scalar1=0.4 * (r - 1.5), scalar2=None, op0=ALU.is_ge)
             halves = (slice(0, 2), slice(2, 4))
             for hf in range(2):
-                nc.vector.tensor_scalar(out=nd[:, halves[hf], :], in0=a_[:, halves[hf], :], scalar1=2.0, scalar2=2.0,
-                                        op0=ALU.min, op1=ALU.subtract)
+                if c not in D_ACT:
+                    nc.vector.tensor_scalar(out=nd[:, halves[hf], :], in0=a_[:, halves[hf], :], scalar1=2.0, scalar2=2.0,
+                                            op0=ALU.min, op1=ALU.subtract)
             for hf in range(2):
-                nc.vector.scalar_tensor_tensor(out=qa[:, halves[hf], :], in0=nd[:, halves[hf], :], scalar=0.5,
+                nc.vector.scalar_tensor_tensor(out=qa[:, halves[hf], :], in0=nd[:, halves[hf], :], scalar=0.5 * sg,
                                                in1=sq[:, halves[1 - hf], :], op0=ALU.mult, op1=ALU.mult)
             for hf in range(2):
-                nc.vector.scalar_tensor_tensor(out=pa[:, halves[hf], :], in0=nd[:, halves[hf], :], scalar=-1.0 / 6.0,
+                nc.vector.scalar_tensor_tensor(out=pa[:, halves[hf], :], in0=nd[:, halves[hf], :], scalar=-sg / 6.0,
                                                in1=sq[:, halves[hf], :], op0=ALU.mult, op1=ALU.mult)
             for hf in range(2):
                 nc.vector.scalar_tensor_tensor(out=v[:, halves[hf], :], in0=qa[:, halves[hf], :], scalar=2.0 / 3.0,

@@ -5,6 +5,7 @@ from concourse.masks import make_identity
 
 F32 = mybir.dt.float32
 BF16 = mybir.dt.bfloat16
+I32 = mybir.dt.int32
 U32 = mybir.dt.uint32
 U8 = mybir.dt.uint8
 FP8X4 = mybir.dt.float8_e4m3fn_x4
@@ -18,9 +19,9 @@ FLOPS = 2 * B * K * OUT
 T = B // P
 
 SIZES = (2, 2, 4, 8, 8, 8, 8, 8, 8, 4, 2, 2)
-LOADS = (4, 12, 16, 16, 16)
-D_ACT = (4, 6, 8)
-HALF = K // 2
+LOADS = (4, 12, 16, 32)
+SHARE_ODD = ()
+ROOT = 6.0 ** -0.5
 
 
 def tile_kanlinearnores_v2_t_kernel(tc, x, spline_weight, out):
@@ -36,12 +37,14 @@ def tile_kanlinearnores_v2_t_kernel(tc, x, spline_weight, out):
         keep = ctx.enter_context(tc.tile_pool(name="keep", bufs=1))
         act2 = ctx.enter_context(tc.tile_pool(name="act2", bufs=2))
         act3 = ctx.enter_context(tc.tile_pool(name="act3", bufs=3))
-        dve = ctx.enter_context(tc.tile_pool(name="dve", bufs=2))
+        dve = ctx.enter_context(tc.tile_pool(name="dve", bufs=1))
         small = ctx.enter_context(tc.tile_pool(name="small", bufs=2))
+        small3 = ctx.enter_context(tc.tile_pool(name="small3", bufs=3))
         xt_pool = ctx.enter_context(tc.psum_pool(name="xtp", bufs=4))
         ops_pool = ctx.enter_context(tc.psum_pool(name="ops", bufs=4))
 
         x_nat = keep.tile([P, T, IN], BF16)
+        xp = keep.tile([P, T, IN], BF16)
         w_sb = keep.tile([P, 2, K], BF16)
         lo = 0
         for l, n in enumerate(LOADS):
@@ -52,11 +55,21 @@ def tile_kanlinearnores_v2_t_kernel(tc, x, spline_weight, out):
 
         identf = keep.tile([P, P], F32)
         make_identity(nc, identf[:])
+        wz = keep.tile([P, 2, 2 * OUT], I32, align_bytes=64)
+        for t in range(2):
+            for h in range(2):
+                nc.gpsimd.memset(wz[:, t, h * OUT:(h + 1) * OUT], 0)
+        two_root = keep.tile([P, 1], F32)
+        nc.vector.memset(two_root[:], 0.0)
+        nc.vector.tensor_scalar(out=two_root[:], in0=two_root[:], scalar1=2.0 * ROOT, scalar2=None, op0=ALU.add)
 
-        def clamp(l):
-            lo = sum(LOADS[:l])
-            piece = x_nat[:, lo:lo + LOADS[l], :]
-            nc.vector.tensor_scalar(out=piece, in0=piece, scalar1=-4.0, scalar2=4.0, op0=ALU.max, op1=ALU.min)
+        def permute(l):
+            t0 = sum(LOADS[:l])
+            t1 = t0 + LOADS[l]
+            src = x_nat[:, t0:t1, :].rearrange("p t (j c i) -> p c t j i", c=4, i=4)
+            dst = xp[:, t0:t1, :].rearrange("p t (c j i) -> p c t j i", c=4, i=4)
+            for c in range(4):
+                nc.vector.tensor_scalar(out=dst[:, c], in0=src[:, c], scalar1=-4.0, scalar2=4.0, op0=ALU.max, op1=ALU.min)
 
         st = {}
 
@@ -64,7 +77,10 @@ def tile_kanlinearnores_v2_t_kernel(tc, x, spline_weight, out):
             return 0 <= c < n_chunks
 
         def x_of(c):
-            return x_nat[:, starts[c]:starts[c] + SIZES[c], :].rearrange("p t i -> p (t i)")
+            return xp[:, starts[c]:starts[c] + SIZES[c], :].rearrange("p t i -> p (t i)")
+
+        def shared(c, q):
+            return q == 0 or c in SHARE_ODD
 
         def stage_1(c):
             if not ok(c):
@@ -73,130 +89,153 @@ def tile_kanlinearnores_v2_t_kernel(tc, x, spline_weight, out):
             w = act2.tile([P, 4, cols], F32, name="w", tag="w")
             a_ = act3.tile([P, 4, cols], F32, name="a", tag="a")
             sq = act3.tile([P, 4, cols], F32, name="sq", tag="sq")
+            f = act2.tile([P, 2, cols], F32, name="f", tag="f")
+            f2 = act2.tile([P, 2, cols], F32, name="f2", tag="f2")
             for r in range(4):
                 nc.scalar.activation(out=w[:, r, :], in_=x_of(c), func=ACT.Abs, bias=1.5 - r, scale=2.5)
             for hf in range(2):
                 nc.scalar.activation(out=a_[:, 2 * hf:2 * hf + 2, :], in_=w[:, 2 * hf:2 * hf + 2, :], func=ACT.Abs, bias=-2.0, scale=1.0)
             for hf in range(2):
-                nc.scalar.activation(out=sq[:, 2 * hf:2 * hf + 2, :], in_=a_[:, 2 * hf:2 * hf + 2, :], func=ACT.Square, bias=2.0, scale=-1.0)
-            if c in D_ACT:
-                d = act3.tile([P, 4, cols], F32, name="d", tag="d")
-                for hf in range(2):
-                    nc.scalar.activation(out=d[:, 2 * hf:2 * hf + 2, :], in_=a_[:, 2 * hf:2 * hf + 2, :], func=ACT.Relu, bias=2.0, scale=-1.0)
-                st[("d", c)] = d
-            st[("a", c)], st[("sq", c)] = a_, sq
+                nc.scalar.activation(out=sq[:, 2 * hf:2 * hf + 2, :], in_=a_[:, 2 * hf:2 * hf + 2, :], func=ACT.Square, bias=two_root[:], scale=-ROOT)
+            par = [q for q in range(2) if shared(c, q)]
+            for q in par:
+                nc.scalar.activation(out=f[:, q, :], in_=a_[:, 1 + q, :], func=ACT.Abs, bias=-1.0, scale=1.0)
+            for q in par:
+                nc.scalar.activation(out=f2[:, q, :], in_=f[:, q, :], func=ACT.Square)
+            st[("a", c)], st[("sq", c)], st[("f", c)], st[("f2", c)] = a_, sq, f, f2
 
-        def stage_2a(c):
+        def sides(c):
+            if not ok(c):
+                return
+            k_ = small3.tile([P, 4, SIZES[c] * IN], BF16, name="k", tag="k")
+            for r in range(4):
+                nc.vector.tensor_scalar(out=k_[:, r, :], in0=x_of(c), scalar1=0.4 * (r - 1.5), scalar2=0.5, op0=ALU.is_ge, op1=ALU.subtract)
+            st[("k", c)] = k_
+
+        def outer(c):
+            if not ok(c):
+                return
+            a_, sq = st[("a", c)], st[("sq", c)]
+            nn = dve.tile([P, 4, SIZES[c] * IN], BF16, name="nn", tag="nn")
+            for hf in range(2):
+                nc.vector.scalar_tensor_tensor(out=nn[:, 2 * hf:2 * hf + 2, :], in0=a_[:, 2 * hf:2 * hf + 2, :], scalar=2.0,
+                                               in1=sq[:, 2 * hf:2 * hf + 2, :], op0=ALU.subtract, op1=ALU.mult)
+            st[("nn", c)] = nn
+
+        def inner(c):
+            if not ok(c):
+                return
+            a_, sq, f, f2 = st[("a", c)], st[("sq", c)], st[("f", c)], st[("f2", c)]
+            mm = dve.tile([P, 4, SIZES[c] * IN], F32, name="mm", tag="mm")
+            for q in range(2):
+                if shared(c, q):
+                    nc.vector.scalar_tensor_tensor(out=mm[:, q, :], in0=f[:, q, :], scalar=2.0, in1=f2[:, q, :], op0=ALU.subtract, op1=ALU.mult)
+                else:
+                    for r in (q, q + 2):
+                        nc.vector.scalar_tensor_tensor(out=mm[:, r, :], in0=a_[:, r, :], scalar=2.0, in1=sq[:, 2 * q + 2 - r, :],
+                                                       op0=ALU.subtract, op1=ALU.mult)
+            st[("mm", c)] = mm
+
+        def rounded(c):
             if not ok(c):
                 return
             cols = SIZES[c] * IN
-            a_, sq = st[("a", c)], st[("sq", c)]
-            m = small.tile([P, 4, cols], BF16, name="m", tag="m")
-            v = small.tile([P, 4, cols], BF16, name="v", tag="v")
-            sg = 1.0
-            if c in D_ACT:
-                nd = st[("d", c)]
-                sg = -1.0
-            else:
-                nd = dve.tile([P, 4, cols], F32, name="nd", tag="nd")
-            qa = dve.tile([P, 4, cols], F32, name="qa", tag="qa")
-            pa = dve.tile([P, 4, cols], F32, name="pa", tag="pa")
-            for r in range(4):
-                nc.vector.tensor_scalar(out=m[:, r, :], in0=x_of(c), scalar1=0.4 * (r - 1.5), scalar2=None, op0=ALU.is_ge)
-            halves = (slice(0, 2), slice(2, 4))
+            nn, mm = st[("nn", c)], st[("mm", c)]
+            pp = dve.tile([P, 4, cols], BF16, name="pp", tag="pp")
+            qq = dve.tile([P, 4, cols], BF16, name="qq", tag="qq")
             for hf in range(2):
-                if c not in D_ACT:
-                    nc.vector.tensor_scalar(out=nd[:, halves[hf], :], in0=a_[:, halves[hf], :], scalar1=2.0, scalar2=2.0,
-                                            op0=ALU.min, op1=ALU.subtract)
-            for hf in range(2):
-                nc.vector.scalar_tensor_tensor(out=qa[:, halves[hf], :], in0=nd[:, halves[hf], :], scalar=0.5 * sg,
-                                               in1=sq[:, halves[1 - hf], :], op0=ALU.mult, op1=ALU.mult)
-            for hf in range(2):
-                nc.vector.scalar_tensor_tensor(out=pa[:, halves[hf], :], in0=nd[:, halves[hf], :], scalar=-sg / 6.0,
-                                               in1=sq[:, halves[hf], :], op0=ALU.mult, op1=ALU.mult)
-            for hf in range(2):
-                nc.vector.scalar_tensor_tensor(out=v[:, halves[hf], :], in0=qa[:, halves[hf], :], scalar=2.0 / 3.0,
-                                               in1=pa[:, halves[hf], :], op0=ALU.add, op1=ALU.min)
-            st[("m", c)], st[("v", c)] = m, v
+                nc.vector.tensor_scalar(out=pp[:, 2 * hf:2 * hf + 2, :], in0=nn[:, 2 * hf:2 * hf + 2, :], scalar1=-1.0, scalar2=0.0,
+                                        op0=ALU.mult, op1=ALU.max)
+            for q in range(2):
+                if shared(c, q):
+                    nc.vector.tensor_scalar(out=qq[:, q, :], in0=mm[:, q, :], scalar1=0.5, scalar2=2.0 / 3.0, op0=ALU.mult, op1=ALU.add)
+                else:
+                    nc.vector.tensor_scalar(out=qq[:, q::2, :], in0=mm[:, q::2, :], scalar1=3.0, scalar2=2.0 / 3.0, op0=ALU.mult, op1=ALU.add)
+            st[("pp", c)], st[("qq", c)] = pp, qq
 
-        def stage_2b(c):
+        def lesser(c):
+            if not ok(c):
+                return
+            pp, qq = st[("pp", c)], st[("qq", c)]
+            v = small.tile([P, 4, SIZES[c] * IN], BF16, name="v", tag="v")
+            for q in range(2):
+                if shared(c, q):
+                    for r in (q, q + 2):
+                        nc.vector.tensor_tensor(out=v[:, r, :], in0=qq[:, q, :], in1=pp[:, r, :], op=ALU.min)
+                else:
+                    nc.vector.tensor_tensor(out=v[:, q::2, :], in0=qq[:, q::2, :], in1=pp[:, q::2, :], op=ALU.min)
+            st[("v", c)] = v
+
+        def signed(c, part):
             if not ok(c):
                 return
             n = SIZES[c]
-            m, v = st[("m", c)], st[("v", c)]
-            pq = small.tile([P, 2, n, HALF], BF16, name="pq", tag="pq")
-            vv = v[:].rearrange("p r (c i) -> p c r i", i=4)
-            mv = m[:].rearrange("p r (c i) -> p c r i", i=4)
-            hi = pq[:, 1].rearrange("p t (q r i) -> p (t q) r i", r=4, i=4)
-            lo_ = pq[:, 0].rearrange("p t (q r i) -> p (t q) r i", r=4, i=4)
-            nq = n * 16
-            parts = (slice(0, nq // 2), slice(nq // 2, nq))
-            for s in parts:
-                nc.vector.tensor_tensor(out=hi[:, s], in0=vv[:, s], in1=mv[:, s], op=ALU.mult)
-            for s in parts:
-                nc.vector.tensor_tensor(out=lo_[:, s], in0=vv[:, s], in1=hi[:, s], op=ALU.subtract)
-            st[("pq", c)] = pq
+            if part == 0:
+                st[("s", c)] = small.tile([P, n, 4 * IN], BF16, name="s", tag="s")
+            half = slice(part * n * 8, (part + 1) * n * 8)
+            sv = st[("s", c)][:].rearrange("p t (q r i) -> p (t q) r i", r=4, i=4)
+            vv = st[("v", c)][:].rearrange("p r (c i) -> p c r i", i=4)
+            kv = st[("k", c)][:].rearrange("p r (c i) -> p c r i", i=4)
+            nc.vector.tensor_tensor(out=sv[:, half], in0=vv[:, half], in1=kv[:, half], op=ALU.mult)
 
-        def stage_3(c):
-            if c not in st_n:
+        def turned(c):
+            if not ok(c):
                 return
-            n, pq = st_n[c], st[("pq", c)]
-            banks = []
-            for j in range(n // 2):
+            pairs, s_ = SIZES[c] // 2, st[("s", c)]
+            sT = small.tile([P, pairs * 2 * P], F32, name="sT", tag="sT")
+            for b in range(0, pairs, 2):
+                k = min(2, pairs - b)
                 xt = xt_pool.tile([P, 2, 2, P], F32, name="xt", tag="xt")
-                for t in range(2):
+                for j in range(k):
+                    words = s_[:, 2 * (b + j):2 * (b + j) + 2, :].rearrange("p t f -> p (t f)").bitcast(F32)
                     for u in range(2):
-                        nc.tensor.transpose(xt[:, t, u, :], pq[:, u, 2 * j + t, :].bitcast(F32), identf[:])
-                banks.append(xt)
-            st[("xt", c)] = banks
+                        nc.tensor.transpose(xt[:, j, u, :], words[:, u::2], identf[:])
+                nc.scalar.copy(out=sT[:, b * 2 * P:(b + k) * 2 * P].rearrange("p (j r u) -> p j r u", j=k, u=2),
+                               in_=xt[:, :k].rearrange("p j u r -> p j r u"))
+            st[("sT", c)] = sT
 
-        def stage_4(c):
-            if c not in st_n:
+        def halves(c):
+            if not ok(c):
                 return
-            n = st_n[c]
-            grouped = small.tile([P, n * K], BF16, name="grouped", tag="grouped", align_bytes=64)
-            g32 = grouped[:].bitcast(F32)
-            for j, xt in enumerate(st[("xt", c)]):
-                nc.scalar.copy(out=g32[:, j * K:(j + 1) * K].rearrange("p (t b u) -> p t b u", t=2, u=2),
-                               in_=xt[:].rearrange("p t u b -> p t b u"))
+            grouped = small.tile([P, 2, SIZES[c] * 2 * P], BF16, name="grouped", tag="grouped", align_bytes=64)
+            sb = st[("sT", c)][:].bitcast(BF16)
+            for h in range(2):
+                nc.vector.tensor_scalar(out=grouped[:, h, :], in0=sb, scalar1=4.0 * h - 2.0, scalar2=0.0, op0=ALU.mult, op1=ALU.max)
             st[("grouped", c)] = grouped
 
-        def stage_5(c):
-            if c not in st_n:
-                return
-            n = st_n[c]
-            if c == "w":
-                codes = keep.tile([P, n * P], U32, name="wcodes", align_bytes=64)
-                scales = keep.tile([P, n * P], U8, name="wscales", align_bytes=64)
-            else:
-                codes = small.tile([P, n * P], U32, name="codes", tag="codes", align_bytes=64)
-                scales = small.tile([P, n * P], U8, name="scales", tag="scales", align_bytes=64)
-            nc.vector.quantize_mx(out=codes[:].bitcast(FP8X4), scales=scales[:], in_=st[("grouped", c)][:])
-            st[("codes", c)], st[("scales", c)] = codes, scales
-
-        def stage_6(c):
+        def quantised(c):
             if not ok(c):
                 return
             n = SIZES[c]
+            codes = small.tile([P, n * P], U32, name="codes", tag="codes", align_bytes=64)
+            scales = small.tile([P, n * P], U8, name="scales", tag="scales", align_bytes=64)
+            nc.vector.quantize_mx(out=codes[:].bitcast(FP8X4), scales=scales[:], in_=st[("grouped", c)][:].rearrange("p h w -> p (h w)"))
+            st[("codes", c)], st[("scales", c)] = codes, scales
+
+        def products(c):
+            if not ok(c):
+                return
+            pairs = SIZES[c] // 2
             codes, scales = st[("codes", c)], st[("scales", c)]
             banks = []
-            for j in range(n // 2):
+            for j in range(pairs):
                 ops = ops_pool.tile([P, 2, OUT], F32, name="ops", tag="ops")
                 for e in range(2):
-                    t = 2 * j + e
-                    nc.tensor.matmul_mx(
-                        out=ops[:, e, :],
-                        lhsT=codes[:, t * P:(t + 1) * P].bitcast(FP8X4),
-                        lhsT_scale=scales[:, t * P:(t + 1) * P],
-                        rhs=st[("codes", "w")][:].bitcast(FP8X4),
-                        rhs_scale=st[("scales", "w")][:],
-                        start=True,
-                        stop=True,
-                    )
+                    for h in range(2):
+                        at = (h * pairs + j) * P
+                        nc.tensor.matmul_mx(
+                            out=ops[:, e, :],
+                            lhsT=codes[:, at:at + P].bitcast(FP8X4),
+                            lhsT_scale=scales[:, at:at + P],
+                            rhs=wz[:, e, h * OUT:(h + 1) * OUT].bitcast(FP8X4),
+                            rhs_scale=st["wscales"][:, h * OUT:(h + 1) * OUT],
+                            start=(h == 0),
+                            stop=(h == 1),
+                        )
                 banks.append(ops)
             st[("banks", c)] = banks
 
-        def stage_7(c):
+        def stored(c):
             if not ok(c):
                 return
             t0, n = starts[c], SIZES[c]
@@ -205,35 +244,60 @@ def tile_kanlinearnores_v2_t_kernel(tc, x, spline_weight, out):
                 nc.scalar.copy(out=out_sb[:, 2 * j:2 * j + 2, :], in_=ops[:])
             nc.sync.dma_start(out=out_v[:, t0:t0 + n, :], in_=out_sb[:])
 
-        st_n = {"w": 2}
-        for c in range(n_chunks):
-            st_n[c] = SIZES[c]
-
         def weights_rows():
-            wpq = keep.tile([P, 2, 2, HALF], BF16)
-            src = w_sb[:].rearrange("p a (q i h r) -> p h a q r i", q=16, i=4, h=2, r=4)
-            for h in range(2):
-                for a in range(2):
-                    nc.vector.tensor_copy(out=wpq[:, h, a, :].rearrange("p (q r i) -> p q r i", r=4, i=4), in_=src[:, h, a])
-            st[("pq", "w")] = wpq
+            wr = keep.tile([P, 2, 2, 2, 4 * IN], BF16)
+            src = w_sb[:].rearrange("p a (j c i h r) -> p a h c j r i", c=4, i=4, h=2, r=4)
+            for a in range(2):
+                for h in range(2):
+                    for c in range(4):
+                        nc.vector.tensor_copy(out=wr[:, a, h, 0, 64 * c:64 * c + 64].rearrange("p (j r i) -> p j r i", r=4, i=4), in_=src[:, a, h, c])
+            flat = wr[:].rearrange("p a h t f -> p (a h) t f")
+            nc.vector.tensor_copy(out=flat[:, :, 1, :], in_=flat[:, :, 0, :])
+            st["wr"] = wr
 
-        clamp(0)
+        def weights_turn():
+            wgrouped = keep.tile([P, 2 * OUT * 4], BF16, align_bytes=64)
+            g32 = wgrouped[:].bitcast(F32)
+            for h in range(2):
+                wt = xt_pool.tile([P, 2, OUT], F32, name="wt", tag="xt")
+                for u in range(2):
+                    for a in range(2):
+                        words = st["wr"][:, a, h].rearrange("p t f -> p (t f)").bitcast(F32)
+                        nc.tensor.transpose(wt[:, u, a * P:(a + 1) * P], words[:, u::2], identf[:])
+                nc.scalar.copy(out=g32[:, h * 2 * OUT:(h + 1) * 2 * OUT].rearrange("p (o u) -> p o u", u=2),
+                               in_=wt[:].rearrange("p u o -> p o u"))
+            st["wgrouped"] = wgrouped
+
+        def weights_codes():
+            wcodes = keep.tile([P, 2 * OUT], U32, align_bytes=64)
+            wscales = keep.tile([P, 2 * OUT], U8, align_bytes=64)
+            nc.vector.quantize_mx(out=wcodes[:].bitcast(FP8X4), scales=wscales[:], in_=st["wgrouped"][:])
+            for t in range(2):
+                nc.vector.tensor_copy(out=wz[64 * t:64 * t + 64, t, :], in_=wcodes[64 * t:64 * t + 64, :].bitcast(I32))
+            st["wscales"] = wscales
+
+        permute(0)
         stage_1(0)
         weights_rows()
-        stage_3("w")
-        clamp(1)
+        permute(1)
+        sides(0)
         for i in range(0, n_chunks + 2):
-            stage_3(i - 1)
-            stage_6(i - 2)
             stage_1(i + 1)
             if i == 0:
-                stage_4("w")
-            stage_4(i - 1)
-            stage_7(i - 2)
-            stage_2a(i)
+                weights_turn()
+            outer(i)
+            signed(i - 1, 0)
+            inner(i)
+            signed(i - 1, 1)
+            turned(i - 1)
+            rounded(i)
+            halves(i - 2)
+            lesser(i)
+            sides(i + 1)
             if i == 0:
-                stage_5("w")
+                weights_codes()
                 for l in range(2, len(LOADS)):
-                    clamp(l)
-            stage_5(i - 1)
-            stage_2b(i)
+                    permute(l)
+            quantised(i - 2)
+            products(i - 2)
+            stored(i - 2)

@@ -19,7 +19,7 @@ FLOPS = 2 * B * K * OUT
 T = B // P
 
 SIZES = (2, 2, 4, 8, 8, 8, 8, 8, 8, 4, 2, 2)
-LOADS = (4, 12, 16, 32)
+LOADS = (4, 28, 32)
 SHARE_ODD = ()
 ROOT = 6.0 ** -0.5
 
@@ -95,11 +95,12 @@ def tile_kanlinearnores_v2_t_kernel(tc, x, spline_weight, out):
                 nc.scalar.activation(out=w[:, r, :], in_=x_of(c), func=ACT.Abs, bias=1.5 - r, scale=2.5)
             for hf in range(2):
                 nc.scalar.activation(out=a_[:, 2 * hf:2 * hf + 2, :], in_=w[:, 2 * hf:2 * hf + 2, :], func=ACT.Abs, bias=-2.0, scale=1.0)
+            par = [q for q in range(2) if shared(c, q)]
             for hf in range(2):
                 nc.scalar.activation(out=sq[:, 2 * hf:2 * hf + 2, :], in_=a_[:, 2 * hf:2 * hf + 2, :], func=ACT.Square, bias=two_root[:], scale=-ROOT)
-            par = [q for q in range(2) if shared(c, q)]
-            for q in par:
-                nc.scalar.activation(out=f[:, q, :], in_=a_[:, 1 + q, :], func=ACT.Abs, bias=-1.0, scale=1.0)
+                if hf == 0:
+                    for q in par:
+                        nc.scalar.activation(out=f[:, q, :], in_=a_[:, 1 + q, :], func=ACT.Abs, bias=-1.0, scale=1.0)
             for q in par:
                 nc.scalar.activation(out=f2[:, q, :], in_=f[:, q, :], func=ACT.Square)
             st[("a", c)], st[("sq", c)], st[("f", c)], st[("f2", c)] = a_, sq, f, f2
@@ -117,9 +118,7 @@ def tile_kanlinearnores_v2_t_kernel(tc, x, spline_weight, out):
                 return
             a_, sq = st[("a", c)], st[("sq", c)]
             nn = dve.tile([P, 4, SIZES[c] * IN], BF16, name="nn", tag="nn")
-            for hf in range(2):
-                nc.vector.scalar_tensor_tensor(out=nn[:, 2 * hf:2 * hf + 2, :], in0=a_[:, 2 * hf:2 * hf + 2, :], scalar=2.0,
-                                               in1=sq[:, 2 * hf:2 * hf + 2, :], op0=ALU.subtract, op1=ALU.mult)
+            nc.vector.scalar_tensor_tensor(out=nn[:], in0=a_[:], scalar=2.0, in1=sq[:], op0=ALU.subtract, op1=ALU.mult)
             st[("nn", c)] = nn
 
         def inner(c):
@@ -143,9 +142,7 @@ def tile_kanlinearnores_v2_t_kernel(tc, x, spline_weight, out):
             nn, mm = st[("nn", c)], st[("mm", c)]
             pp = dve.tile([P, 4, cols], BF16, name="pp", tag="pp")
             qq = dve.tile([P, 4, cols], BF16, name="qq", tag="qq")
-            for hf in range(2):
-                nc.vector.tensor_scalar(out=pp[:, 2 * hf:2 * hf + 2, :], in0=nn[:, 2 * hf:2 * hf + 2, :], scalar1=-1.0, scalar2=0.0,
-                                        op0=ALU.mult, op1=ALU.max)
+            nc.vector.tensor_scalar(out=pp[:], in0=nn[:], scalar1=-1.0, scalar2=0.0, op0=ALU.mult, op1=ALU.max)
             for q in range(2):
                 if shared(c, q):
                     nc.vector.tensor_scalar(out=qq[:, q, :], in0=mm[:, q, :], scalar1=0.5, scalar2=2.0 / 3.0, op0=ALU.mult, op1=ALU.add)
@@ -160,23 +157,22 @@ def tile_kanlinearnores_v2_t_kernel(tc, x, spline_weight, out):
             v = small.tile([P, 4, SIZES[c] * IN], BF16, name="v", tag="v")
             for q in range(2):
                 if shared(c, q):
-                    for r in (q, q + 2):
-                        nc.vector.tensor_tensor(out=v[:, r, :], in0=qq[:, q, :], in1=pp[:, r, :], op=ALU.min)
+                    both = qq[:, q:q + 1, :].to_broadcast([P, 2, SIZES[c] * IN])
+                    nc.vector.tensor_tensor(out=v[:, q::2, :], in0=both, in1=pp[:, q::2, :], op=ALU.min)
                 else:
                     nc.vector.tensor_tensor(out=v[:, q::2, :], in0=qq[:, q::2, :], in1=pp[:, q::2, :], op=ALU.min)
             st[("v", c)] = v
 
-        def signed(c, part):
+        def signed(c):
             if not ok(c):
                 return
             n = SIZES[c]
-            if part == 0:
-                st[("s", c)] = small.tile([P, n, 4 * IN], BF16, name="s", tag="s")
-            half = slice(part * n * 8, (part + 1) * n * 8)
-            sv = st[("s", c)][:].rearrange("p t (q r i) -> p (t q) r i", r=4, i=4)
+            s_ = small.tile([P, n, 4 * IN], BF16, name="s", tag="s")
+            sv = s_[:].rearrange("p t (q r i) -> p (t q) r i", r=4, i=4)
             vv = st[("v", c)][:].rearrange("p r (c i) -> p c r i", i=4)
             kv = st[("k", c)][:].rearrange("p r (c i) -> p c r i", i=4)
-            nc.vector.tensor_tensor(out=sv[:, half], in0=vv[:, half], in1=kv[:, half], op=ALU.mult)
+            nc.vector.tensor_tensor(out=sv, in0=vv, in1=kv, op=ALU.mult)
+            st[("s", c)] = s_
 
         def turned(c):
             if not ok(c):
@@ -264,7 +260,7 @@ def tile_kanlinearnores_v2_t_kernel(tc, x, spline_weight, out):
                     for a in range(2):
                         words = st["wr"][:, a, h].rearrange("p t f -> p (t f)").bitcast(F32)
                         nc.tensor.transpose(wt[:, u, a * P:(a + 1) * P], words[:, u::2], identf[:])
-                nc.scalar.copy(out=g32[:, h * 2 * OUT:(h + 1) * 2 * OUT].rearrange("p (o u) -> p o u", u=2),
+                nc.vector.tensor_copy(out=g32[:, h * 2 * OUT:(h + 1) * 2 * OUT].rearrange("p (o u) -> p o u", u=2),
                                in_=wt[:].rearrange("p u o -> p o u"))
             st["wgrouped"] = wgrouped
 
@@ -286,9 +282,8 @@ def tile_kanlinearnores_v2_t_kernel(tc, x, spline_weight, out):
             if i == 0:
                 weights_turn()
             outer(i)
-            signed(i - 1, 0)
+            signed(i - 1)
             inner(i)
-            signed(i - 1, 1)
             turned(i - 1)
             rounded(i)
             halves(i - 2)

@@ -19,7 +19,7 @@ FLOPS = 2 * B * K * OUT
 T = B // P
 
 SIZES = (2, 2, 4, 8, 8, 8, 8, 8, 8, 4, 2, 2)
-LOADS = (4, 28, 32)
+LOADS = (4, 12, 48)
 SHARE_ODD = ()
 ROOT = 6.0 ** -0.5
 
@@ -39,9 +39,9 @@ def tile_kanlinearnores_v2_t_kernel(tc, x, spline_weight, out):
         act3 = ctx.enter_context(tc.tile_pool(name="act3", bufs=3))
         dve = ctx.enter_context(tc.tile_pool(name="dve", bufs=1))
         small = ctx.enter_context(tc.tile_pool(name="small", bufs=2))
-        small3 = ctx.enter_context(tc.tile_pool(name="small3", bufs=3))
-        xt_pool = ctx.enter_context(tc.psum_pool(name="xtp", bufs=4))
-        ops_pool = ctx.enter_context(tc.psum_pool(name="ops", bufs=4))
+        small5 = ctx.enter_context(tc.tile_pool(name="small5", bufs=5))
+        xt_pool = ctx.enter_context(tc.psum_pool(name="xtp", bufs=3))
+        ops_pool = ctx.enter_context(tc.psum_pool(name="ops", bufs=5))
 
         x_nat = keep.tile([P, T, IN], BF16)
         xp = keep.tile([P, T, IN], BF16)
@@ -50,15 +50,17 @@ def tile_kanlinearnores_v2_t_kernel(tc, x, spline_weight, out):
         for l, n in enumerate(LOADS):
             nc.sync.dma_start(out=x_nat[:, lo:lo + n, :], in_=x_v[:, lo:lo + n, :])
             lo += n
-            if l == 0:
+            if l == 1:
                 nc.sync.dma_start(out=w_sb[:], in_=w_v)
 
         identf = keep.tile([P, P], F32)
         make_identity(nc, identf[:])
-        wz = keep.tile([P, 2, 2 * OUT], I32, align_bytes=64)
-        for t in range(2):
-            for h in range(2):
-                nc.gpsimd.memset(wz[:, t, h * OUT:(h + 1) * OUT], 0)
+        wz = keep.tile([P, 2, 2, OUT], I32, align_bytes=64)
+        for h in range(2):
+            for t in range(2):
+                nc.gpsimd.memset(wz[:, h, t, :], 0)
+        wscales = keep.tile([P, 2, 2, OUT], U8, align_bytes=64)
+        nc.gpsimd.memset(wscales[:].bitcast(I32), 0)
         two_root = keep.tile([P, 1], F32)
         nc.vector.memset(two_root[:], 0.0)
         nc.vector.tensor_scalar(out=two_root[:], in0=two_root[:], scalar1=2.0 * ROOT, scalar2=None, op0=ALU.add)
@@ -108,7 +110,7 @@ def tile_kanlinearnores_v2_t_kernel(tc, x, spline_weight, out):
         def sides(c):
             if not ok(c):
                 return
-            k_ = small3.tile([P, 4, SIZES[c] * IN], BF16, name="k", tag="k")
+            k_ = small5.tile([P, 4, SIZES[c] * IN], BF16, name="k", tag="k")
             for r in range(4):
                 nc.vector.tensor_scalar(out=k_[:, r, :], in0=x_of(c), scalar1=0.4 * (r - 1.5), scalar2=0.5, op0=ALU.is_ge, op1=ALU.subtract)
             st[("k", c)] = k_
@@ -216,18 +218,17 @@ def tile_kanlinearnores_v2_t_kernel(tc, x, spline_weight, out):
             banks = []
             for j in range(pairs):
                 ops = ops_pool.tile([P, 2, OUT], F32, name="ops", tag="ops")
-                for e in range(2):
-                    for h in range(2):
-                        at = (h * pairs + j) * P
-                        nc.tensor.matmul_mx(
-                            out=ops[:, e, :],
-                            lhsT=codes[:, at:at + P].bitcast(FP8X4),
-                            lhsT_scale=scales[:, at:at + P],
-                            rhs=wz[:, e, h * OUT:(h + 1) * OUT].bitcast(FP8X4),
-                            rhs_scale=st["wscales"][:, h * OUT:(h + 1) * OUT],
-                            start=(h == 0),
-                            stop=(h == 1),
-                        )
+                for h in range(2):
+                    at = (h * pairs + j) * P
+                    nc.tensor.matmul_mx(
+                        out=ops[:].rearrange("p t o -> p (t o)"),
+                        lhsT=codes[:, at:at + P].bitcast(FP8X4),
+                        lhsT_scale=scales[:, at:at + P],
+                        rhs=wz[:, h].rearrange("p t o -> p (t o)").bitcast(FP8X4),
+                        rhs_scale=wscales[:, h].rearrange("p t o -> p (t o)"),
+                        start=(h == 0),
+                        stop=(h == 1),
+                    )
                 banks.append(ops)
             st[("banks", c)] = banks
 
@@ -237,7 +238,10 @@ def tile_kanlinearnores_v2_t_kernel(tc, x, spline_weight, out):
             t0, n = starts[c], SIZES[c]
             out_sb = small.tile([P, n, OUT], F32, name="out_sb", tag="out_sb")
             for j, ops in enumerate(st[("banks", c)]):
-                nc.scalar.copy(out=out_sb[:, 2 * j:2 * j + 2, :], in_=ops[:])
+                if c >= n_chunks - 2:
+                    nc.vector.tensor_copy(out=out_sb[:, 2 * j:2 * j + 2, :], in_=ops[:])
+                else:
+                    nc.scalar.copy(out=out_sb[:, 2 * j:2 * j + 2, :], in_=ops[:])
             nc.sync.dma_start(out=out_v[:, t0:t0 + n, :], in_=out_sb[:])
 
         def weights_rows():
@@ -266,17 +270,21 @@ def tile_kanlinearnores_v2_t_kernel(tc, x, spline_weight, out):
 
         def weights_codes():
             wcodes = keep.tile([P, 2 * OUT], U32, align_bytes=64)
-            wscales = keep.tile([P, 2 * OUT], U8, align_bytes=64)
-            nc.vector.quantize_mx(out=wcodes[:].bitcast(FP8X4), scales=wscales[:], in_=st["wgrouped"][:])
+            wc = wcodes[:].rearrange("p (h o) -> p h o", h=2)
+            for h in range(2):
+                nc.vector.quantize_mx(out=wcodes[:, h * OUT:(h + 1) * OUT].bitcast(FP8X4), scales=wscales[:, h, 0, :],
+                                      in_=st["wgrouped"][:, h * 4 * OUT:(h + 1) * 4 * OUT])
+            nc.vector.tensor_copy(out=wscales[:, :, 1, :].bitcast(I32), in_=wscales[:, :, 0, :].bitcast(I32))
             for t in range(2):
-                nc.vector.tensor_copy(out=wz[64 * t:64 * t + 64, t, :], in_=wcodes[64 * t:64 * t + 64, :].bitcast(I32))
-            st["wscales"] = wscales
+                nc.vector.tensor_copy(out=wz[64 * t:64 * t + 64, :, t, :], in_=wc[64 * t:64 * t + 64].bitcast(I32))
 
         permute(0)
         stage_1(0)
-        weights_rows()
         permute(1)
         sides(0)
+        weights_rows()
+        sides(1)
+        sides(2)
         for i in range(0, n_chunks + 2):
             stage_1(i + 1)
             if i == 0:
@@ -288,7 +296,7 @@ def tile_kanlinearnores_v2_t_kernel(tc, x, spline_weight, out):
             rounded(i)
             halves(i - 2)
             lesser(i)
-            sides(i + 1)
+            sides(i + 3)
             if i == 0:
                 weights_codes()
                 for l in range(2, len(LOADS)):

@@ -35,8 +35,8 @@ def tile_kanlinearnores_v2_t_kernel(tc, x, spline_weight, out):
 
     with ExitStack() as ctx:
         keep = ctx.enter_context(tc.tile_pool(name="keep", bufs=1))
-        act2 = ctx.enter_context(tc.tile_pool(name="act2", bufs=2))
-        act3 = ctx.enter_context(tc.tile_pool(name="act3", bufs=3))
+        act1 = ctx.enter_context(tc.tile_pool(name="act1", bufs=1))
+        act4 = ctx.enter_context(tc.tile_pool(name="act4", bufs=4))
         dve = ctx.enter_context(tc.tile_pool(name="dve", bufs=1))
         small = ctx.enter_context(tc.tile_pool(name="small", bufs=2))
         small5 = ctx.enter_context(tc.tile_pool(name="small5", bufs=5))
@@ -88,11 +88,11 @@ def tile_kanlinearnores_v2_t_kernel(tc, x, spline_weight, out):
             if not ok(c):
                 return
             cols = SIZES[c] * IN
-            w = act2.tile([P, 4, cols], F32, name="w", tag="w")
-            a_ = act3.tile([P, 4, cols], F32, name="a", tag="a")
-            sq = act3.tile([P, 4, cols], F32, name="sq", tag="sq")
-            f = act2.tile([P, 2, cols], F32, name="f", tag="f")
-            f2 = act2.tile([P, 2, cols], F32, name="f2", tag="f2")
+            w = act1.tile([P, 4, cols], F32, name="w", tag="w")
+            a_ = act4.tile([P, 4, cols], F32, name="a", tag="a")
+            sq = act4.tile([P, 4, cols], F32, name="sq", tag="sq")
+            f = act4.tile([P, 1, cols], F32, name="f", tag="f")
+            f2 = act4.tile([P, 1, cols], F32, name="f2", tag="f2")
             for r in range(4):
                 nc.scalar.activation(out=w[:, r, :], in_=x_of(c), func=ACT.Abs, bias=1.5 - r, scale=2.5)
             for hf in range(2):

@@ -84,8 +84,19 @@ def tile_kanlinearnores_v2_t_kernel(tc, x, spline_weight, out):
         def shared(c, q):
             return q == 0 or c in SHARE_ODD
 
-        def stage_1(c):
+        def front(c, part):
             if not ok(c):
+                return
+            par = [q for q in range(2) if shared(c, q)]
+            if part == 1:
+                a_, sq, f, f2 = st[("a", c)], st[("sq", c)], st[("f", c)], st[("f2", c)]
+                for hf in range(2):
+                    nc.scalar.activation(out=sq[:, 2 * hf:2 * hf + 2, :], in_=a_[:, 2 * hf:2 * hf + 2, :], func=ACT.Square, bias=two_root[:], scale=-ROOT)
+                    if hf == 0:
+                        for q in par:
+                            nc.scalar.activation(out=f[:, q, :], in_=a_[:, 1 + q, :], func=ACT.Abs, bias=-1.0, scale=1.0)
+                for q in par:
+                    nc.scalar.activation(out=f2[:, q, :], in_=f[:, q, :], func=ACT.Square)
                 return
             cols = SIZES[c] * IN
             w = act1.tile([P, 4, cols], F32, name="w", tag="w")
@@ -97,14 +108,6 @@ def tile_kanlinearnores_v2_t_kernel(tc, x, spline_weight, out):
                 nc.scalar.activation(out=w[:, r, :], in_=x_of(c), func=ACT.Abs, bias=1.5 - r, scale=2.5)
             for hf in range(2):
                 nc.scalar.activation(out=a_[:, 2 * hf:2 * hf + 2, :], in_=w[:, 2 * hf:2 * hf + 2, :], func=ACT.Abs, bias=-2.0, scale=1.0)
-            par = [q for q in range(2) if shared(c, q)]
-            for hf in range(2):
-                nc.scalar.activation(out=sq[:, 2 * hf:2 * hf + 2, :], in_=a_[:, 2 * hf:2 * hf + 2, :], func=ACT.Square, bias=two_root[:], scale=-ROOT)
-                if hf == 0:
-                    for q in par:
-                        nc.scalar.activation(out=f[:, q, :], in_=a_[:, 1 + q, :], func=ACT.Abs, bias=-1.0, scale=1.0)
-            for q in par:
-                nc.scalar.activation(out=f2[:, q, :], in_=f[:, q, :], func=ACT.Square)
             st[("a", c)], st[("sq", c)], st[("f", c)], st[("f2", c)] = a_, sq, f, f2
 
         def sides(c):
@@ -180,7 +183,7 @@ def tile_kanlinearnores_v2_t_kernel(tc, x, spline_weight, out):
             if not ok(c):
                 return
             pairs, s_ = SIZES[c] // 2, st[("s", c)]
-            sT = small.tile([P, pairs * 2 * P], F32, name="sT", tag="sT")
+            st[("xt", c)] = []
             for b in range(0, pairs, 2):
                 k = min(2, pairs - b)
                 xt = xt_pool.tile([P, 2, 2, P], F32, name="xt", tag="xt")
@@ -188,6 +191,13 @@ def tile_kanlinearnores_v2_t_kernel(tc, x, spline_weight, out):
                     words = s_[:, 2 * (b + j):2 * (b + j) + 2, :].rearrange("p t f -> p (t f)").bitcast(F32)
                     for u in range(2):
                         nc.tensor.transpose(xt[:, j, u, :], words[:, u::2], identf[:])
+                st[("xt", c)].append((b, k, xt))
+
+        def words_out(c):
+            if not ok(c):
+                return
+            sT = small.tile([P, SIZES[c] * P], F32, name="sT", tag="sT")
+            for b, k, xt in st[("xt", c)]:
                 nc.scalar.copy(out=sT[:, b * 2 * P:(b + k) * 2 * P].rearrange("p (j r u) -> p j r u", j=k, u=2),
                                in_=xt[:, :k].rearrange("p j u r -> p j r u"))
             st[("sT", c)] = sT
@@ -278,29 +288,36 @@ def tile_kanlinearnores_v2_t_kernel(tc, x, spline_weight, out):
             for t in range(2):
                 nc.vector.tensor_copy(out=wz[64 * t:64 * t + 64, :, t, :], in_=wc[64 * t:64 * t + 64].bitcast(I32))
 
+        ctx.enter_context(tc.manual_schedule(engines={mybir.EngineType.Activation}))
         permute(0)
-        stage_1(0)
+        front(0, 0)
+        front(0, 1)
         permute(1)
         sides(0)
         weights_rows()
         sides(1)
         sides(2)
+        front(1, 0)
+        front(1, 1)
         for i in range(0, n_chunks + 2):
-            stage_1(i + 1)
+            outer(i)
             if i == 0:
                 weights_turn()
-            outer(i)
             signed(i - 1)
-            inner(i)
             turned(i - 1)
+            inner(i)
             rounded(i)
             halves(i - 2)
             lesser(i)
-            sides(i + 3)
             if i == 0:
-                weights_codes()
                 for l in range(2, len(LOADS)):
                     permute(l)
+            sides(i + 3)
             quantised(i - 2)
+            if i == 0:
+                weights_codes()
             products(i - 2)
+            front(i + 2, 0)
+            words_out(i - 1)
+            front(i + 2, 1)
             stored(i - 2)

@@ -18,9 +18,9 @@ K = IN * NB
 FLOPS = 2 * B * K * OUT
 T = B // P
 
-SIZES = (2, 2, 4, 8, 8, 8, 8, 8, 8, 4, 2, 2)
+SIZES = (4, 4, 8, 8, 8, 8, 8, 8, 4, 2, 2)
 LOADS = (4, 12, 48)
-SHARE_ODD = ()
+SHARE_ODD = (8, 9, 10)
 ROOT = 6.0 ** -0.5
 
 
@@ -102,8 +102,8 @@ def tile_kanlinearnores_v2_t_kernel(tc, x, spline_weight, out):
             w = act1.tile([P, 4, cols], F32, name="w", tag="w")
             a_ = act4.tile([P, 4, cols], F32, name="a", tag="a")
             sq = act4.tile([P, 4, cols], F32, name="sq", tag="sq")
-            f = act4.tile([P, 1, cols], F32, name="f", tag="f")
-            f2 = act4.tile([P, 1, cols], F32, name="f2", tag="f2")
+            f = act4.tile([P, len(par), cols], F32, name="f", tag="f")
+            f2 = act4.tile([P, len(par), cols], F32, name="f2", tag="f2")
             for r in range(4):
                 nc.scalar.activation(out=w[:, r, :], in_=x_of(c), func=ACT.Abs, bias=1.5 - r, scale=2.5)
             for hf in range(2):

from contextlib import ExitStack

import concourse.mybir as mybir
from concourse.masks import make_identity

F32 = mybir.dt.float32
BF16 = mybir.dt.bfloat16
I32 = mybir.dt.int32
U32 = mybir.dt.uint32
U8 = mybir.dt.uint8
FP8X4 = mybir.dt.float8_e4m3fn_x4
ALU = mybir.AluOpType
ACT = mybir.ActivationFunctionType

P = 128
B, IN, OUT, NB = 8192, 64, 256, 8
K = IN * NB
FLOPS = 2 * B * K * OUT
T = B // P

SIZES = (4, 4, 8, 8, 8, 8, 8, 8, 4, 2, 2)
LOADS = (4, 12, 48)
SHARE_ODD = (8, 9, 10)
ROOT = 6.0 ** -0.5


def tile_kanlinearnores_v2_t_kernel(tc, x, spline_weight, out):
    nc = tc.nc
    x_v = x.rearrange("(p t) i -> p t i", t=T)
    w_v = spline_weight.rearrange("(a p) i g -> p a (i g)", p=P)
    out_v = out.rearrange("(p t) o -> p t o", t=T)
    n_chunks = len(SIZES)
    starts = [sum(SIZES[:c]) for c in range(n_chunks)]
    assert sum(SIZES) == T and sum(LOADS) == T

    with ExitStack() as ctx:
        keep = ctx.enter_context(tc.tile_pool(name="keep", bufs=1))
        act1 = ctx.enter_context(tc.tile_pool(name="act1", bufs=1))
        act4 = ctx.enter_context(tc.tile_pool(name="act4", bufs=4))
        dve = ctx.enter_context(tc.tile_pool(name="dve", bufs=1))
        small = ctx.enter_context(tc.tile_pool(name="small", bufs=2))
        small5 = ctx.enter_context(tc.tile_pool(name="small5", bufs=5))
        xt_pool = ctx.enter_context(tc.psum_pool(name="xtp", bufs=3))
        ops_pool = ctx.enter_context(tc.psum_pool(name="ops", bufs=5))

        x_nat = keep.tile([P, T, IN], BF16)
        xp = keep.tile([P, T, IN], BF16)
        w_sb = keep.tile([P, 2, K], BF16)
        lo = 0
        for l, n in enumerate(LOADS):
            nc.sync.dma_start(out=x_nat[:, lo:lo + n, :], in_=x_v[:, lo:lo + n, :])
            lo += n
            if l == 1:
                nc.sync.dma_start(out=w_sb[:], in_=w_v)

        identf = keep.tile([P, P], F32)
        make_identity(nc, identf[:])
        wz = keep.tile([P, 2, 2, OUT], I32, align_bytes=64)
        for h in range(2):
            for t in range(2):
                nc.gpsimd.memset(wz[:, h, t, :], 0)
        wscales = keep.tile([P, 2, 2, OUT], U8, align_bytes=64)
        nc.gpsimd.memset(wscales[:].bitcast(I32), 0)
        two_root = keep.tile([P, 1], F32)
        nc.vector.memset(two_root[:], 0.0)
        nc.vector.tensor_scalar(out=two_root[:], in0=two_root[:], scalar1=2.0 * ROOT, scalar2=None, op0=ALU.add)

        def permute(l):
            t0 = sum(LOADS[:l])
            t1 = t0 + LOADS[l]
            src = x_nat[:, t0:t1, :].rearrange("p t (j c i) -> p c t j i", c=4, i=4)
            dst = xp[:, t0:t1, :].rearrange("p t (c j i) -> p c t j i", c=4, i=4)
            for c in range(4):
                nc.vector.tensor_scalar(out=dst[:, c], in0=src[:, c], scalar1=-4.0, scalar2=4.0, op0=ALU.max, op1=ALU.min)

        st = {}

        def ok(c):
            return 0 <= c < n_chunks

        def x_of(c):
            return xp[:, starts[c]:starts[c] + SIZES[c], :].rearrange("p t i -> p (t i)")

        def shared(c, q):
            return q == 0 or c in SHARE_ODD

        def front(c, part):
            if not ok(c):
                return
            par = [q for q in range(2) if shared(c, q)]
            if part == 1:
                a_, sq, f, f2 = st[("a", c)], st[("sq", c)], st[("f", c)], st[("f2", c)]
                for hf in range(2):
                    nc.scalar.activation(out=sq[:, 2 * hf:2 * hf + 2, :], in_=a_[:, 2 * hf:2 * hf + 2, :], func=ACT.Square, bias=two_root[:], scale=-ROOT)
                    if hf == 0:
                        for q in par:
                            nc.scalar.activation(out=f[:, q, :], in_=a_[:, 1 + q, :], func=ACT.Abs, bias=-1.0, scale=1.0)
                for q in par:
                    nc.scalar.activation(out=f2[:, q, :], in_=f[:, q, :], func=ACT.Square)
                return
            cols = SIZES[c] * IN
            w = act1.tile([P, 4, cols], F32, name="w", tag="w")
            a_ = act4.tile([P, 4, cols], F32, name="a", tag="a")
            sq = act4.tile([P, 4, cols], F32, name="sq", tag="sq")
            f = act4.tile([P, len(par), cols], F32, name="f", tag="f")
            f2 = act4.tile([P, len(par), cols], F32, name="f2", tag="f2")
            for r in range(4):
                nc.scalar.activation(out=w[:, r, :], in_=x_of(c), func=ACT.Abs, bias=1.5 - r, scale=2.5)
            for hf in range(2):
                nc.scalar.activation(out=a_[:, 2 * hf:2 * hf + 2, :], in_=w[:, 2 * hf:2 * hf + 2, :], func=ACT.Abs, bias=-2.0, scale=1.0)
            st[("a", c)], st[("sq", c)], st[("f", c)], st[("f2", c)] = a_, sq, f, f2

        def sides(c):
            if not ok(c):
                return
            k_ = small5.tile([P, 4, SIZES[c] * IN], BF16, name="k", tag="k")
            for r in range(4):
                nc.vector.tensor_scalar(out=k_[:, r, :], in0=x_of(c), scalar1=0.4 * (r - 1.5), scalar2=0.5, op0=ALU.is_ge, op1=ALU.subtract)
            st[("k", c)] = k_

        def outer(c):
            if not ok(c):
                return
            a_, sq = st[("a", c)], st[("sq", c)]
            nn = dve.tile([P, 4, SIZES[c] * IN], BF16, name="nn", tag="nn")
            nc.vector.scalar_tensor_tensor(out=nn[:], in0=a_[:], scalar=2.0, in1=sq[:], op0=ALU.subtract, op1=ALU.mult)
            st[("nn", c)] = nn

        def inner(c):
            if not ok(c):
                return
            a_, sq, f, f2 = st[("a", c)], st[("sq", c)], st[("f", c)], st[("f2", c)]
            mm = dve.tile([P, 4, SIZES[c] * IN], F32, name="mm", tag="mm")
            for q in range(2):
                if shared(c, q):
                    nc.vector.scalar_tensor_tensor(out=mm[:, q, :], in0=f[:, q, :], scalar=2.0, in1=f2[:, q, :], op0=ALU.subtract, op1=ALU.mult)
                else:
                    for r in (q, q + 2):
                        nc.vector.scalar_tensor_tensor(out=mm[:, r, :], in0=a_[:, r, :], scalar=2.0, in1=sq[:, 2 * q + 2 - r, :],
                                                       op0=ALU.subtract, op1=ALU.mult)
            st[("mm", c)] = mm

        def rounded(c):
            if not ok(c):
                return
            cols = SIZES[c] * IN
            nn, mm = st[("nn", c)], st[("mm", c)]
            pp = dve.tile([P, 4, cols], BF16, name="pp", tag="pp")
            qq = dve.tile([P, 4, cols], BF16, name="qq", tag="qq")
            nc.vector.tensor_scalar(out=pp[:], in0=nn[:], scalar1=-1.0, scalar2=0.0, op0=ALU.mult, op1=ALU.max)
            for q in range(2):
                if shared(c, q):
                    nc.vector.tensor_scalar(out=qq[:, q, :], in0=mm[:, q, :], scalar1=0.5, scalar2=2.0 / 3.0, op0=ALU.mult, op1=ALU.add)
                else:
                    nc.vector.tensor_scalar(out=qq[:, q::2, :], in0=mm[:, q::2, :], scalar1=3.0, scalar2=2.0 / 3.0, op0=ALU.mult, op1=ALU.add)
            st[("pp", c)], st[("qq", c)] = pp, qq

        def lesser(c):
            if not ok(c):
                return
            pp, qq = st[("pp", c)], st[("qq", c)]
            v = small.tile([P, 4, SIZES[c] * IN], BF16, name="v", tag="v")
            for q in range(2):
                if shared(c, q):
                    both = qq[:, q:q + 1, :].to_broadcast([P, 2, SIZES[c] * IN])
                    nc.vector.tensor_tensor(out=v[:, q::2, :], in0=both, in1=pp[:, q::2, :], op=ALU.min)
                else:
                    nc.vector.tensor_tensor(out=v[:, q::2, :], in0=qq[:, q::2, :], in1=pp[:, q::2, :], op=ALU.min)
            st[("v", c)] = v

        def signed(c):
            if not ok(c):
                return
            n = SIZES[c]
            s_ = small.tile([P, n, 4 * IN], BF16, name="s", tag="s")
            sv = s_[:].rearrange("p t (q r i) -> p (t q) r i", r=4, i=4)
            vv = st[("v", c)][:].rearrange("p r (c i) -> p c r i", i=4)
            kv = st[("k", c)][:].rearrange("p r (c i) -> p c r i", i=4)
            nc.vector.tensor_tensor(out=sv, in0=vv, in1=kv, op=ALU.mult)
            st[("s", c)] = s_

        def turned(c):
            if not ok(c):
                return
            pairs, s_ = SIZES[c] // 2, st[("s", c)]
            st[("xt", c)] = []
            for b in range(0, pairs, 2):
                k = min(2, pairs - b)
                xt = xt_pool.tile([P, 2, 2, P], F32, name="xt", tag="xt")
                for j in range(k):
                    words = s_[:, 2 * (b + j):2 * (b + j) + 2, :].rearrange("p t f -> p (t f)").bitcast(F32)
                    for u in range(2):
                        nc.tensor.transpose(xt[:, j, u, :], words[:, u::2], identf[:])
                st[("xt", c)].append((b, k, xt))

        def words_out(c):
            if not ok(c):
                return
            sT = small.tile([P, SIZES[c] * P], F32, name="sT", tag="sT")
            for b, k, xt in st[("xt", c)]:
                nc.scalar.copy(out=sT[:, b * 2 * P:(b + k) * 2 * P].rearrange("p (j r u) -> p j r u", j=k, u=2),
                               in_=xt[:, :k].rearrange("p j u r -> p j r u"))
            st[("sT", c)] = sT

        def halves(c):
            if not ok(c):
                return
            grouped = small.tile([P, 2, SIZES[c] * 2 * P], BF16, name="grouped", tag="grouped", align_bytes=64)
            sb = st[("sT", c)][:].bitcast(BF16)
            for h in range(2):
                nc.vector.tensor_scalar(out=grouped[:, h, :], in0=sb, scalar1=4.0 * h - 2.0, scalar2=0.0, op0=ALU.mult, op1=ALU.max)
            st[("grouped", c)] = grouped

        def quantised(c):
            if not ok(c):
                return
            n = SIZES[c]
            codes = small.tile([P, n * P], U32, name="codes", tag="codes", align_bytes=64)
            scales = small.tile([P, n * P], U8, name="scales", tag="scales", align_bytes=64)
            nc.vector.quantize_mx(out=codes[:].bitcast(FP8X4), scales=scales[:], in_=st[("grouped", c)][:].rearrange("p h w -> p (h w)"))
            st[("codes", c)], st[("scales", c)] = codes, scales

        def products(c):
            if not ok(c):
                return
            pairs = SIZES[c] // 2
            codes, scales = st[("codes", c)], st[("scales", c)]
            banks = []
            for j in range(pairs):
                ops = ops_pool.tile([P, 2, OUT], F32, name="ops", tag="ops")
                for h in range(2):
                    at = (h * pairs + j) * P
                    nc.tensor.matmul_mx(
                        out=ops[:].rearrange("p t o -> p (t o)"),
                        lhsT=codes[:, at:at + P].bitcast(FP8X4),
                        lhsT_scale=scales[:, at:at + P],
                        rhs=wz[:, h].rearrange("p t o -> p (t o)").bitcast(FP8X4),
                        rhs_scale=wscales[:, h].rearrange("p t o -> p (t o)"),
                        start=(h == 0),
                        stop=(h == 1),
                    )
                banks.append(ops)
            st[("banks", c)] = banks

        def stored(c):
            if not ok(c):
                return
            t0, n = starts[c], SIZES[c]
            out_sb = small.tile([P, n, OUT], F32, name="out_sb", tag="out_sb")
            for j, ops in enumerate(st[("banks", c)]):
                if c >= n_chunks - 2:
                    nc.vector.tensor_copy(out=out_sb[:, 2 * j:2 * j + 2, :], in_=ops[:])
                else:
                    nc.scalar.copy(out=out_sb[:, 2 * j:2 * j + 2, :], in_=ops[:])
            nc.sync.dma_start(out=out_v[:, t0:t0 + n, :], in_=out_sb[:])

        def weights_rows():
            wr = keep.tile([P, 2, 2, 2, 4 * IN], BF16)
            src = w_sb[:].rearrange("p a (j c i h r) -> p a h c j r i", c=4, i=4, h=2, r=4)
            for a in range(2):
                for h in range(2):
                    for c in range(4):
                        nc.vector.tensor_copy(out=wr[:, a, h, 0, 64 * c:64 * c + 64].rearrange("p (j r i) -> p j r i", r=4, i=4), in_=src[:, a, h, c])
            flat = wr[:].rearrange("p a h t f -> p (a h) t f")
            nc.vector.tensor_copy(out=flat[:, :, 1, :], in_=flat[:, :, 0, :])
            st["wr"] = wr

        def weights_turn():
            wgrouped = keep.tile([P, 2 * OUT * 4], BF16, align_bytes=64)
            g32 = wgrouped[:].bitcast(F32)
            for h in range(2):
                wt = xt_pool.tile([P, 2, OUT], F32, name="wt", tag="xt")
                for u in range(2):
                    for a in range(2):
                        words = st["wr"][:, a, h].rearrange("p t f -> p (t f)").bitcast(F32)
                        nc.tensor.transpose(wt[:, u, a * P:(a + 1) * P], words[:, u::2], identf[:])
                nc.vector.tensor_copy(out=g32[:, h * 2 * OUT:(h + 1) * 2 * OUT].rearrange("p (o u) -> p o u", u=2),
                               in_=wt[:].rearrange("p u o -> p o u"))
            st["wgrouped"] = wgrouped

        def weights_codes():
            wcodes = keep.tile([P, 2 * OUT], U32, align_bytes=64)
            wc = wcodes[:].rearrange("p (h o) -> p h o", h=2)
            for h in range(2):
                nc.vector.quantize_mx(out=wcodes[:, h * OUT:(h + 1) * OUT].bitcast(FP8X4), scales=wscales[:, h, 0, :],
                                      in_=st["wgrouped"][:, h * 4 * OUT:(h + 1) * 4 * OUT])
            nc.vector.tensor_copy(out=wscales[:, :, 1, :].bitcast(I32), in_=wscales[:, :, 0, :].bitcast(I32))
            for t in range(2):
                nc.vector.tensor_copy(out=wz[64 * t:64 * t + 64, :, t, :], in_=wc[64 * t:64 * t + 64].bitcast(I32))

        ctx.enter_context(tc.manual_schedule(engines={mybir.EngineType.Activation}))
        permute(0)
        front(0, 0)
        front(0, 1)
        permute(1)
        sides(0)
        weights_rows()
        sides(1)
        sides(2)
        front(1, 0)
        front(1, 1)
        for i in range(0, n_chunks + 2):
            outer(i)
            if i == 0:
                weights_turn()
            signed(i - 1)
            turned(i - 1)
            inner(i)
            rounded(i)
            halves(i - 2)
            lesser(i)
            if i == 0:
                for l in range(2, len(LOADS)):
                    permute(l)
            sides(i + 3)
            quantised(i - 2)
            if i == 0:
                weights_codes()
            products(i - 2)
            front(i + 2, 0)
            words_out(i - 1)
            front(i + 2, 1)
            stored(i - 2)
